import numpy as np
import ml_dtypes


def mxq(x, axis, fmt="e4m3"):
    dtype, down = {"e4m3": (ml_dtypes.float8_e4m3fn, 7), "e5m2": (ml_dtypes.float8_e5m2, 14)}[fmt]
    v = np.moveaxis(np.asarray(x, np.float32).astype(ml_dtypes.bfloat16).astype(np.float64), axis, -1)
    blocks = v.reshape(v.shape[:-1] + (-1, 32))
    amax = np.abs(blocks).max(-1, keepdims=True)
    byte = np.maximum(np.where(amax > 0, np.frexp(amax)[1] - 1 + 127, 0) - down, 1)
    scale = np.exp2(byte - 127.0)
    codes = (blocks / scale).astype(np.float32).astype(dtype).astype(np.float64)
    return np.moveaxis((codes * scale).reshape(v.shape), -1, axis)


WIDE = False


def mx_kscale(k):
    if not WIDE:
        return np.ones(k)
    levels = np.array([10, -10, 5, -5, 0])
    if k % 512:
        return np.exp2(np.random.permutation(np.resize(levels, k // 32))).repeat(32)
    a = np.empty((k // 512, 16))
    for p in range(k // 512):
        a[p, :8] = np.random.permutation(np.resize(levels, 8))
        for g in range(8):
            far = levels[np.abs(levels - a[p, g]) >= 10]
            a[p, g + 8] = far[np.random.randint(len(far))]
    return np.exp2(a.ravel()).repeat(32)


BF16 = ml_dtypes.bfloat16


def bf(x):
    return np.asarray(x, np.float32).astype(BF16)


def f64(x):
    return np.asarray(x).astype(np.float64)


B, S, D, H, DH, DL, DR = 2, 1024, 8192, 16, 128, 2048, 64
ROPE_BASE = 10000.0


def rope_cos_sin():
    inv_freq = 1.0 / ROPE_BASE ** (np.arange(0, DR, 2) / DR)
    freqs = np.arange(S)[:, None] * inv_freq[None, :]
    emb = np.concatenate([freqs, freqs], axis=-1)
    return np.cos(emb)[None, :, None, :], np.sin(emb)[None, :, None, :]


def rotate_half(u):
    u1, u2 = np.split(u, 2, axis=-1)
    return np.concatenate([-u2, u1], axis=-1)


def setup_inputs():
    s, t = mx_kscale(D), mx_kscale(DL)
    return {"x": bf(np.random.standard_normal((B, S, D)) * s),
            "W_kv_down": bf(np.random.standard_normal((D, DL)) / np.sqrt(D) / s[:, None] * t),
            "W_kv_up": bf(np.random.standard_normal((DL, H * (DH + DR + DH))) / np.sqrt(DL) / t[:, None])}


def reference(x, W_kv_down, W_kv_up):
    kv_latent = mxq(f64(x), 2, "e4m3") @ mxq(f64(W_kv_down), 0, "e4m3")
    kv_full = (mxq(kv_latent, 2, "e4m3") @ mxq(f64(W_kv_up), 0, "e4m3")).reshape(B, S, H, DH + DR + DH)
    k_content = kv_full[..., :DH]
    k_rope = kv_full[..., DH:DH + DR]
    v = kv_full[..., DH + DR:]
    cos, sin = rope_cos_sin()
    k_rope = k_rope * cos + rotate_half(k_rope) * sin
    k = np.concatenate([k_content, k_rope], axis=-1)
    return k, v

@@ -1,0 +1,452 @@
+from contextlib import ExitStack
+
+import concourse.mybir as mybir
+from concourse.masks import make_identity
+
+FLOPS = 2 * 2048 * 8192 * 2048 + 2 * 2048 * 2048 * 5120
+
+F32 = mybir.dt.float32
+BF16 = mybir.dt.bfloat16
+U32 = mybir.dt.uint32
+I32 = mybir.dt.int32
+U8 = mybir.dt.uint8
+FP8 = mybir.dt.float8_e4m3fn_x4
+ALU = mybir.AluOpType
+ACT = mybir.ActivationFunctionType
+
+P = 128
+TWO_PI = 6.283185307179586
+
+XC = 0
+XS = 131072
+LC = 139264
+LS = 172032
+WC = 174080
+WS = 215040
+WR = 217600
+GR = 225792
+LB = 238080
+ID = 242176
+MISC = 242688
+XR = LC + 8192
+WR0 = XC + 3 * 32768
+GR0 = XC + 2 * 32768
+UR = 0
+UC0 = 20480
+US0 = 40960
+COSF = 42496
+SINF = 50688
+TMP = 58880
+UCN = 65536
+
+
+def tile_multilatentattention_pa_l_kernel(tc, x, w_down, w_up, out_k, out_v):
+    nc = tc.nc
+    xf = x.flatten_outer_dims()
+    kf = out_k.rearrange("b s h d -> (b s) (h d)")
+    vf = out_v.rearrange("b s h d -> (b s) (h d)")
+
+    with ExitStack() as ctx:
+        sbp = ctx.enter_context(tc.tile_pool(name="sb", bufs=1))
+        psp = ctx.enter_context(tc.psum_pool(name="ps", bufs=1))
+        ctx.enter_context(tc.manual_schedule())
+
+        def sb(shape, dtype, off, tag):
+            return sbp.tile(shape, dtype, name=tag, tag=tag, offset=off, align_bytes=64)
+
+        def bank(shape, k):
+            return psp.tile(shape, F32, name="b%d" % k, tag="b%d" % k)
+
+        def cp(eng, out, in_):
+            if eng == "V":
+                nc.vector.tensor_copy(out=out, in_=in_)
+            else:
+                nc.scalar.copy(out=out, in_=in_)
+
+        st = {"gr": 0, "lb": 0, "lq": 0}
+        xr, tb, grx, xc, xs = {}, {}, {}, {}, {}
+        wr, grw, wc, ws = {}, {}, {}, {}
+        acc, lbt, grl, lc, ls = {}, {}, {}, {}, {}
+        ur, uc, us = {}, {}, {}
+
+        ident = sb([P, P], F32, ID, "ident")
+        make_identity(nc, ident[:])
+
+        chi = sb([P, 32], F32, MISC, "chi")
+        cmid = sb([P, 32], F32, MISC + 128, "cmid")
+        clo = sb([P, 32], F32, MISC + 256, "clo")
+        posi = sb([P, 8], I32, MISC + 384, "posi")
+        posf = sb([P, 8], F32, MISC + 448, "posf")
+        for i in range(32):
+            c = 10000.0 ** (-i / 32.0) / TWO_PI
+            hi = int(c * 65536.0) / 65536.0
+            mid = int((c - hi) * 1073741824.0) / 1073741824.0
+            lo = int((c - hi - mid) * 18014398509481984.0) / 18014398509481984.0
+            nc.gpsimd.memset(chi[:, i:i + 1], hi)
+            nc.gpsimd.memset(cmid[:, i:i + 1], mid)
+            nc.gpsimd.memset(clo[:, i:i + 1], lo)
+        nc.gpsimd.iota(posi[:], pattern=[[128, 8]], base=0, channel_multiplier=1)
+
+        FIRST = -2
+        LAST1 = 80
+
+        def need_w(G, a):
+            return 2 * a if G == 0 else 32 + 16 * (G - 1) + 2 * a
+
+        w_at = {}
+        for b in range(FIRST - 1, LAST1):
+            w_at[b] = []
+        for G in range(4):
+            for g in range(16):
+                a, gl = divmod(g, 4)
+                if G == 0:
+                    e = 2 * a - 2 + gl // 2
+                elif a == 0:
+                    e = (10 + 4 * gl) if G == 1 else need_w(G, 0) - 15 + 2 * gl
+                else:
+                    e = need_w(G, 0) - 6 + (10 * (4 * (a - 1) + gl)) // 12
+                w_at[e].append((G, g))
+        order_w = []
+        for b in range(FIRST, LAST1):
+            order_w.extend(w_at[b])
+
+        def new_gr(b):
+            k = st["gr"]
+            st["gr"] = k + 1
+            if b < 8:
+                return sb([P, 2048], BF16, GR0 + 4096 * (k % 8), "gra%d" % (k % 8))
+            n = 3 if b < 32 else 2
+            return sb([P, 2048], BF16, GR + 4096 * (k % n), "gr%d" % (k % n))
+
+        def load_x(n):
+            c, hq = divmod(n, 8)
+            t = sb([P, 4, 1024], BF16, XR + 8192 * (n % 3), "xr%d" % (n % 3))
+            src = xf[512 * c:512 * (c + 1), 1024 * hq:1024 * (hq + 1)].rearrange("(i p) k -> p i k", p=P)
+            if n == 0:
+                for i in range(4):
+                    nc.sync.dma_start(out=t[:, i, :], in_=src[:, i, :])
+            else:
+                nc.sync.dma_start(out=t[:], in_=src)
+            xr[n] = t
+
+        def transposes(n):
+            for g2 in range(2):
+                for hb in range(2):
+                    t = bank([P, 2, 256], 4 + 2 * g2 + hb)
+                    for i2 in range(2):
+                        words = xr[n][:, 2 * hb + i2, :].bitcast(F32)
+                        for u in range(2):
+                            nc.tensor.transpose(
+                                t[:, u, 128 * i2:128 * (i2 + 1)],
+                                words[:, 256 * g2 + u:256 * (g2 + 1):2],
+                                ident[:],
+                            )
+                    tb[(n, g2, hb)] = t
+
+        def copy_x(n, g2, hb, eng, b):
+            if (n, g2) not in grx:
+                grx[(n, g2)] = new_gr(b)
+            gw = grx[(n, g2)][:].bitcast(F32).rearrange("p (r u) -> p r u", u=2)
+            cp(eng, gw[:, 256 * hb:256 * (hb + 1), :], tb[(n, g2, hb)][:].rearrange("p u r -> p r u"))
+
+        def quant_x(n, g2):
+            c, hq = divmod(n, 8)
+            a, h = divmod(hq, 2)
+            gl = 2 * h + g2
+            if (c, a) not in xc:
+                xc[(c, a)] = sb([P, 4, 512], U32, XC + 8192 * (4 * c + a), "xc%d" % (4 * c + a))
+                xs[(c, a)] = sb([P, 512], U8, XS + 512 * (4 * c + a), "xs%d" % (4 * c + a))
+            nc.vector.quantize_mx(
+                out=xc[(c, a)][:, gl, :].bitcast(FP8), scales=xs[(c, a)][4 * gl:P, :], in_=grx[(n, g2)][:]
+            )
+
+        def load_w(k):
+            G, g = order_w[k]
+            if G == 0:
+                t = sb([P, 4, 512], BF16, WR0 + 4096 * (k % 8), "wra%d" % (k % 8))
+            else:
+                t = sb([P, 4, 512], BF16, WR + 4096 * (k % 2), "wr%d" % (k % 2))
+            nc.sync.dma_start(
+                out=t[:],
+                in_=w_down[512 * g:512 * (g + 1), 512 * G:512 * (G + 1)].rearrange("(p j) c -> p j c", j=4),
+            )
+            wr[(G, g)] = t
+
+        def inter_w(G, g, eng, b):
+            t = new_gr(b)
+            grw[(G, g)] = t
+            cp(
+                eng,
+                t[:].rearrange("p (t m j) -> p t m j", t=4, j=4),
+                wr[(G, g)][:].rearrange("p j (m t) -> p t m j", t=4),
+            )
+            k = order_w.index((G, g))
+            if k < 10:
+                load_w(k + 6)
+            elif k >= 14 and k + 2 < 64:
+                load_w(k + 2)
+
+        def quant_w(G, g):
+            a, gl = divmod(g, 4)
+            if (G, a) not in wc:
+                s = (4 * G + a) % 5
+                wc[(G, a)] = sb([P, 4, 512], U32, WC + 8192 * s, "wc%d" % s)
+                ws[(G, a)] = sb([P, 512], U8, WS + 512 * s, "ws%d" % s)
+            nc.vector.quantize_mx(
+                out=wc[(G, a)][:, gl, :].bitcast(FP8), scales=ws[(G, a)][4 * gl:P, :], in_=grw[(G, g)][:]
+            )
+
+        def mm1(G, c, a, t, k):
+            if a == 0:
+                acc[(G, c, t)] = bank([P, 512], k)
+            for gl in range(4):
+                nc.tensor.matmul_mx(
+                    out=acc[(G, c, t)][:],
+                    lhsT=wc[(G, a)][:, gl, 128 * t:128 * (t + 1)].bitcast(FP8),
+                    lhsT_scale=ws[(G, a)][4 * gl:P, 128 * t:128 * (t + 1)],
+                    rhs=xc[(c, a)][:, gl, :].bitcast(FP8),
+                    rhs_scale=xs[(c, a)][4 * gl:P, :],
+                    start=(a == 0 and gl == 0),
+                    stop=(a == 3 and gl == 3),
+                )
+
+        def evac_lat(G, c, t, eng, b):
+            if (G, c) not in lbt:
+                k = st["lb"]
+                st["lb"] = k + 1
+                if b < 32 or k % 2 == 0:
+                    lbt[(G, c)] = sb([P, 4, 512], BF16, LB, "lb0")
+                else:
+                    lbt[(G, c)] = sb([P, 4, 512], BF16, GR + 8192, "lb1")
+            cp(eng, lbt[(G, c)][:, t, :], acc[(G, c, t)][:])
+
+        def inter_lat(G, c, b):
+            t = new_gr(b)
+            grl[(G, c)] = t
+            nc.vector.tensor_copy(
+                out=t[:].rearrange("p (r t) -> p r t", t=4), in_=lbt[(G, c)][:].rearrange("p t r -> p r t")
+            )
+
+        def quant_lat(G, c):
+            lc[(G, c)] = sb([P, 512], U32, LC + 2048 * (4 * G + c), "lc%d" % (4 * G + c))
+            if c not in ls:
+                ls[c] = sb([P, 512], U8, LS + 512 * c, "ls%d" % c)
+            nc.vector.quantize_mx(out=lc[(G, c)][:].bitcast(FP8), scales=ls[c][4 * G:P, :], in_=grl[(G, c)][:])
+
+        def load_u(k):
+            Q, G = divmod(k, 4)
+            t = sb([P, 4, 1280], BF16, UR + 10240 * (k % 2), "ur%d" % (k % 2))
+            nc.sync.dma_start(
+                out=t[:],
+                in_=w_up[512 * G:512 * (G + 1), 1280 * Q:1280 * (Q + 1)].rearrange("(p j) c -> p j c", j=4),
+            )
+            ur[(Q, G)] = t
+
+        PARTS = ((0, 128, 0), (192, 128, 512), (128, 64, 1024))
+
+        def prep_u(Q, G, part, eng, b):
+            f0, nf, c0 = PARTS[part]
+            t = new_gr(b)
+            src = ur[(Q, G)][:].rearrange("p j (h w) -> p h w j", h=4)[:, :, f0:f0 + nf, :]
+            cp(eng, t[:, 0:16 * nf].rearrange("p (h m j) -> p h m j", h=4, j=4), src)
+            return t
+
+        def quant_u(Q, G, part, t):
+            f0, nf, c0 = PARTS[part]
+            if Q not in uc:
+                base = UC0 if Q == 0 else UCN + 22016 * (Q - 1)
+                uc[Q] = sb([P, 4, 1280], U32, base, "uc%d" % Q)
+                us[Q] = sb([P, 1280], U8, base + 20480, "us%d" % Q)
+            nc.vector.quantize_mx(
+                out=uc[Q][:, G, c0:c0 + 4 * nf].bitcast(FP8),
+                scales=us[Q][4 * G:P, c0:c0 + 4 * nf],
+                in_=t[:, 0:16 * nf],
+            )
+
+        def unit_u(Q, G, b):
+            t0 = prep_u(Q, G, 0, "V", b)
+            t1 = prep_u(Q, G, 1, "S", b)
+            quant_u(Q, G, 0, t0)
+            t2 = prep_u(Q, G, 2, "V", b)
+            if 4 * Q + G + 2 < 16:
+                load_u(4 * Q + G + 2)
+            quant_u(Q, G, 1, t1)
+            quant_u(Q, G, 2, t2)
+
+        rope = {}
+
+        def rope_tables():
+            nc.vector.tensor_copy(out=posf[:], in_=posi[:])
+            tm = [sb([P, 8, 32], F32, TMP + 1024 * k, "tmp%d" % k) for k in range(5)]
+            ti = sb([P, 8, 32], I32, TMP + 1024 * 5, "tmpi")
+            for s in range(8):
+                nc.vector.tensor_scalar_mul(out=tm[0][:, s, :], in0=chi[:], scalar1=posf[:, s:s + 1])
+                nc.vector.tensor_scalar_mul(out=tm[1][:, s, :], in0=cmid[:], scalar1=posf[:, s:s + 1])
+                nc.vector.tensor_scalar_mul(out=tm[2][:, s, :], in0=clo[:], scalar1=posf[:, s:s + 1])
+            nc.vector.tensor_copy(out=ti[:], in_=tm[0][:])
+            nc.vector.tensor_copy(out=tm[3][:], in_=ti[:])
+            nc.vector.tensor_tensor(out=tm[0][:], in0=tm[0][:], in1=tm[3][:], op=ALU.subtract)
+            nc.vector.tensor_tensor(out=tm[1][:], in0=tm[1][:], in1=tm[2][:], op=ALU.add)
+            nc.vector.tensor_tensor(out=tm[0][:], in0=tm[0][:], in1=tm[1][:], op=ALU.add)
+            nc.vector.tensor_scalar_add(out=tm[1][:], in0=tm[0][:], scalar1=0.25)
+            nc.vector.scalar_tensor_tensor(out=tm[2][:], in0=tm[0][:], scalar=0.5, in1=tm[0][:], op0=ALU.is_gt, op1=ALU.subtract)
+            nc.vector.scalar_tensor_tensor(out=tm[3][:], in0=tm[1][:], scalar=0.5, in1=tm[1][:], op0=ALU.is_gt, op1=ALU.subtract)
+            nc.scalar.activation(out=tm[0][:], in_=tm[2][:], func=ACT.Sin, scale=-TWO_PI)
+            nc.scalar.activation(out=tm[1][:], in_=tm[2][:], func=ACT.Sin, scale=TWO_PI)
+            nc.scalar.activation(out=tm[4][:], in_=tm[3][:], func=ACT.Sin, scale=-TWO_PI)
+            cosf = sb([P, 8, 8, 32], F32, COSF, "cosf")
+            sinf = sb([P, 8, 8, 32], F32, SINF, "sinf")
+            for hh in range(8):
+                nc.vector.tensor_copy(out=cosf[:, :, hh, :], in_=tm[4][:])
+                nc.vector.tensor_copy(out=sinf[:, :, hh, :], in_=tm[1 - hh % 2][:])
+            rope["cos"] = cosf
+            rope["sin"] = sinf
+
+        ot = {}
+
+        def mm2(Q, i):
+            s = 16 * Q + i
+            c, il = divmod(i, 4)
+            tiles = []
+            for part in range(3):
+                f0, nf, c0 = PARTS[part]
+                t = bank([P, 4 * nf], (3 * s + part + 4) % 8)
+                for G in range(4):
+                    nc.tensor.matmul_mx(
+                        out=t[:],
+                        lhsT=lc[(G, c)][:, 128 * il:128 * (il + 1)].bitcast(FP8),
+                        lhsT_scale=ls[c][4 * G:P, 128 * il:128 * (il + 1)],
+                        rhs=uc[Q][:, G, c0:c0 + 4 * nf].bitcast(FP8),
+                        rhs_scale=us[Q][4 * G:P, c0:c0 + 4 * nf],
+                        start=(G == 0),
+                        stop=(G == 3),
+                    )
+                tiles.append(t)
+            ot[s] = tiles
+
+        def evac2(Q, i):
+            s = 16 * Q + i
+            pc, pv, pr = ot[s]
+            base = WC + 8192 * (1 + s % 4)
+            okt = sb([P, 4, 192], F32, base, "ok%d" % (s % 4))
+            ovt = sb([P, 512], F32, base + 3072, "ov%d" % (s % 4))
+            t1 = sb([P, 4, 2, 32], F32, base + 5120, "ta%d" % (s % 4))
+            t2 = sb([P, 4, 2, 32], F32, base + 6144, "tb%d" % (s % 4))
+            nc.scalar.copy(out=okt[:, :, 0:128], in_=pc[:].rearrange("p (h m) -> p h m", h=4))
+            nc.scalar.copy(out=ovt[:], in_=pv[:])
+            prv = pr[:].rearrange("p (h e r) -> p h e r", h=4, e=2)
+            cosv = rope["cos"][:, i % 8, :, :].rearrange("p (h e) r -> p h e r", e=2)
+            sinv = rope["sin"][:, i % 8, :, :].rearrange("p (h e) r -> p h e r", e=2)
+            nc.vector.tensor_tensor(out=t1[:], in0=prv, in1=cosv, op=ALU.mult)
+            nc.vector.tensor_tensor(out=t2[:, :, 0, :], in0=prv[:, :, 1, :], in1=sinv[:, :, 0, :], op=ALU.mult)
+            nc.vector.tensor_tensor(out=t2[:, :, 1, :], in0=prv[:, :, 0, :], in1=sinv[:, :, 1, :], op=ALU.mult)
+            nc.vector.tensor_tensor(
+                out=okt[:, :, 128:192],
+                in0=t1[:].rearrange("p h e r -> p h (e r)"),
+                in1=t2[:].rearrange("p h e r -> p h (e r)"),
+                op=ALU.add,
+            )
+            nc.sync.dma_start(out=vf[128 * i:128 * (i + 1), 512 * Q:512 * (Q + 1)], in_=ovt[:])
+            nc.sync.dma_start(
+                out=kf[128 * i:128 * (i + 1), 768 * Q:768 * (Q + 1)], in_=okt[:].rearrange("p h d -> p (h d)")
+            )
+
+        load_x(0)
+        load_w(0)
+        load_w(1)
+        load_x(1)
+        load_w(2)
+        load_w(3)
+        load_x(2)
+        load_w(4)
+        load_w(5)
+
+        nc.vector.memset(posf[:], 0.0)
+        nc.scalar.copy(out=posf[:], in_=posf[:])
+
+        pend_q = []
+
+        def flush_lat():
+            k = st["lq"]
+            if k < len(pend_q):
+                quant_lat(pend_q[k][0], pend_q[k][1])
+                st["lq"] = k + 1
+
+        for b in range(FIRST, LAST1):
+            head = b < 32
+            units = w_at[b]
+            n = b + 2
+            if head and n < 32:
+                transposes(n)
+            if b >= 0:
+                if head:
+                    c, r = divmod(b, 8)
+                    a, half = divmod(r, 2)
+                    for t in (2 * half, 2 * half + 1):
+                        mm1(0, c, a, t, t)
+                else:
+                    G, r = divmod(b - 32, 16)
+                    G = G + 1
+                    hs, r = divmod(r, 8)
+                    a, cl = divmod(r, 2)
+                    c = 2 * hs + cl
+                    for t in range(4):
+                        mm1(G, c, a, t, 4 * (1 - cl) + t)
+            if head and b + 5 < 32:
+                load_x(b + 5)
+            if head and n < 32:
+                copy_x(n, 0, 0, "V" if b < 8 else "S", b)
+                copy_x(n, 0, 1, "S" if b < 8 else "V", b)
+                copy_x(n, 1, 0, "S", b)
+                copy_x(n, 1, 1, "S" if b < 8 else "V", b)
+                quant_x(n, 0)
+            for k, (wG, wg) in enumerate(units):
+                if head:
+                    eng = "S" if k == 0 else "V"
+                else:
+                    eng = "S" if (wg % 2 == 0) else "V"
+                inter_w(wG, wg, eng, b)
+                if k == 0:
+                    flush_lat()
+                    if head and n < 32:
+                        quant_x(n, 1)
+            if not units:
+                flush_lat()
+                if head and n < 32:
+                    quant_x(n, 1)
+            for (wG, wg) in units:
+                quant_w(wG, wg)
+            if b >= 0:
+                if head:
+                    if a == 3:
+                        for t in (2 * half, 2 * half + 1):
+                            evac_lat(0, c, t, "S", b)
+                        if half == 1:
+                            inter_lat(0, c, b)
+                            pend_q.append((0, c))
+                else:
+                    if a == 3:
+                        for t in range(4):
+                            evac_lat(G, c, t, "S", b)
+                        inter_lat(G, c, b)
+                        pend_q.append((G, c))
+            if b == 71:
+                load_u(0)
+                load_u(1)
+            if b == 72:
+                rope_tables()
+            if b in (73, 74, 76, 77):
+                G2 = (73, 74, 76, 77).index(b)
+                unit_u(0, G2, b)
+        flush_lat()
+        flush_lat()
+
+        for s in range(64):
+            Q, i = divmod(s, 16)
+            mm2(Q, i)
+            if s > 0:
+                evac2((s - 1) // 16, (s - 1) % 16)
+            if Q < 3 and i % 4 == 1:
+                G2 = i // 4
+                unit_u(Q + 1, G2, 100)
+        evac2(3, 15)

@@ -31,6 +31,9 @@ MISC = 242688
 XR = LC + 8192
 WR0 = XC + 3 * 32768
 GR0 = XC + 2 * 32768
+SRT = XC + 3 * 32768 + 16384
+SORT0 = 10
+SORT1 = 32
 UR = 0
 UC0 = 20480
 US0 = 40960
@@ -64,7 +67,7 @@ def tile_multilatentattention_pa_l_kernel(tc, x, w_down, w_up, out_k, out_v):
                 nc.scalar.copy(out=out, in_=in_)
 
         st = {"gr": 0, "lb": 0, "lq": 0}
-        xr, tb, grx, xc, xs = {}, {}, {}, {}, {}
+        xr, xq, tb, grx, xc, xs = {}, {}, {}, {}, {}, {}
         wr, grw, wc, ws = {}, {}, {}, {}
         acc, lbt, grl, lc, ls = {}, {}, {}, {}, {}
         ur, uc, us = {}, {}, {}
@@ -103,6 +106,8 @@ def tile_multilatentattention_pa_l_kernel(tc, x, w_down, w_up, out_k, out_v):
                     e = 2 * a - 2 + gl // 2
                 elif a == 0:
                     e = (10 + 4 * gl) if G == 1 else need_w(G, 0) - 15 + 2 * gl
+                elif G == 1:
+                    e = 30 + 2 * (a - 1) + gl // 2
                 else:
                     e = need_w(G, 0) - 6 + (10 * (4 * (a - 1) + gl)) // 12
                 w_at[e].append((G, g))
@@ -129,6 +134,14 @@ def tile_multilatentattention_pa_l_kernel(tc, x, w_down, w_up, out_k, out_v):
                 nc.sync.dma_start(out=t[:], in_=src)
             xr[n] = t
 
+        def sort_x(n, eng):
+            if n < 30:
+                t = sb([P, 8, 2, 128], F32, SRT + 8192 * (n % 2), "xq%d" % (n % 2))
+            else:
+                t = sb([P, 8, 2, 128], F32, WC + 8192 * (n - 30), "xq%d" % (n - 28))
+            cp(eng, t[:], xr[n][:].rearrange("p i k -> p (i k)").bitcast(F32).rearrange("p (q w u) -> p q u w", u=2, w=128))
+            xq[n] = t
+
         def transposes(n):
             for g2 in range(2):
                 for hb in range(2):
@@ -136,11 +149,11 @@ def tile_multilatentattention_pa_l_kernel(tc, x, w_down, w_up, out_k, out_v):
                     for i2 in range(2):
                         words = xr[n][:, 2 * hb + i2, :].bitcast(F32)
                         for u in range(2):
-                            nc.tensor.transpose(
-                                t[:, u, 128 * i2:128 * (i2 + 1)],
-                                words[:, 256 * g2 + u:256 * (g2 + 1):2],
-                                ident[:],
-                            )
+                            if n in xq:
+                                src = xq[n][:, 2 * (2 * hb + i2) + g2, u, :]
+                            else:
+                                src = words[:, 256 * g2 + u:256 * (g2 + 1):2]
+                            nc.tensor.transpose(t[:, u, 128 * i2:128 * (i2 + 1)], src, ident[:])
                     tb[(n, g2, hb)] = t
 
         def copy_x(n, g2, hb, eng, b):
@@ -164,8 +177,10 @@ def tile_multilatentattention_pa_l_kernel(tc, x, w_down, w_up, out_k, out_v):
             G, g = order_w[k]
             if G == 0:
                 t = sb([P, 4, 512], BF16, WR0 + 4096 * (k % 8), "wra%d" % (k % 8))
-            else:
+            elif k < 20:
                 t = sb([P, 4, 512], BF16, WR + 4096 * (k % 2), "wr%d" % (k % 2))
+            else:
+                t = sb([P, 4, 512], BF16, (WR, WR + 4096, LC + 24576, LC + 28672)[k % 4], "wr%d" % (k % 4))
             nc.sync.dma_start(
                 out=t[:],
                 in_=w_down[512 * g:512 * (g + 1), 512 * G:512 * (G + 1)].rearrange("(p j) c -> p j c", j=4),
@@ -183,8 +198,10 @@ def tile_multilatentattention_pa_l_kernel(tc, x, w_down, w_up, out_k, out_v):
             k = order_w.index((G, g))
             if k < 10:
                 load_w(k + 6)
-            elif k >= 14 and k + 2 < 64:
+            elif 14 <= k < 18:
                 load_w(k + 2)
+            elif 20 <= k < 60:
+                load_w(k + 4)
 
         def quant_w(G, g):
             a, gl = divmod(g, 4)
@@ -308,9 +325,9 @@ def tile_multilatentattention_pa_l_kernel(tc, x, w_down, w_up, out_k, out_v):
             s = 16 * Q + i
             c, il = divmod(i, 4)
             tiles = []
-            for part in range(3):
+            for k, part in enumerate((2, 0, 1)):
                 f0, nf, c0 = PARTS[part]
-                t = bank([P, 4 * nf], (3 * s + part + 4) % 8)
+                t = bank([P, 4 * nf], (3 * s + k + 4) % 8)
                 for G in range(4):
                     nc.tensor.matmul_mx(
                         out=t[:],
@@ -326,7 +343,7 @@ def tile_multilatentattention_pa_l_kernel(tc, x, w_down, w_up, out_k, out_v):
 
         def evac2(Q, i):
             s = 16 * Q + i
-            pc, pv, pr = ot[s]
+            pr, pc, pv = ot[s]
             base = WC + 8192 * (1 + s % 4)
             okt = sb([P, 4, 192], F32, base, "ok%d" % (s % 4))
             ovt = sb([P, 512], F32, base + 3072, "ov%d" % (s % 4))
@@ -394,15 +411,19 @@ def tile_multilatentattention_pa_l_kernel(tc, x, w_down, w_up, out_k, out_v):
                         mm1(G, c, a, t, 4 * (1 - cl) + t)
             if head and b + 5 < 32:
                 load_x(b + 5)
+            if SORT0 <= b + 3 < SORT1:
+                sort_x(b + 3, "S")
             if head and n < 32:
                 copy_x(n, 0, 0, "V" if b < 8 else "S", b)
                 copy_x(n, 0, 1, "S" if b < 8 else "V", b)
                 copy_x(n, 1, 0, "S", b)
                 copy_x(n, 1, 1, "S" if b < 8 else "V", b)
                 quant_x(n, 0)
+            else:
+                flush_lat()
             for k, (wG, wg) in enumerate(units):
                 if head:
-                    eng = "S" if k == 0 else "V"
+                    eng = "S" if (k == 0 and not SORT0 <= b + 3 < SORT1) else "V"
                 else:
                     eng = "S" if (wg % 2 == 0) else "V"
                 inter_w(wG, wg, eng, b)
@@ -410,17 +431,19 @@ def tile_multilatentattention_pa_l_kernel(tc, x, w_down, w_up, out_k, out_v):
                     flush_lat()
                     if head and n < 32:
                         quant_x(n, 1)
-            if not units:
+                else:
+                    quant_w(units[k - 1][0], units[k - 1][1])
+            if units:
+                quant_w(units[-1][0], units[-1][1])
+            else:
                 flush_lat()
                 if head and n < 32:
                     quant_x(n, 1)
-            for (wG, wg) in units:
-                quant_w(wG, wg)
             if b >= 0:
                 if head:
                     if a == 3:
                         for t in (2 * half, 2 * half + 1):
-                            evac_lat(0, c, t, "S", b)
+                            evac_lat(0, c, t, "V" if SORT0 <= b + 3 < SORT1 else "S", b)
                         if half == 1:
                             inter_lat(0, c, b)
                             pend_q.append((0, c))
@@ -430,6 +453,9 @@ def tile_multilatentattention_pa_l_kernel(tc, x, w_down, w_up, out_k, out_v):
                             evac_lat(G, c, t, "S", b)
                         inter_lat(G, c, b)
                         pend_q.append((G, c))
+            if b == 27:
+                for k in range(20, 24):
+                    load_w(k)
             if b == 71:
                 load_u(0)
                 load_u(1)

@@ -18,16 +18,16 @@ P = 128
 TWO_PI = 6.283185307179586
 
 XC = 0
-XS = 131072
-LC = 139264
-LS = 172032
-WC = 174080
-WS = 215040
-WR = 217600
-GR = 225792
-LB = 238080
-ID = 242176
-MISC = 242688
+XS = 131072 + 128
+LC = 139648
+LS = 172608
+WC = 174720
+WS = 215872
+WR = 218432
+GR = 226624
+LB = 238912
+ID = 243008
+MISC = 243520
 XR = LC + 8192
 WR0 = XC + 3 * 32768
 GR0 = XC + 2 * 32768
@@ -273,7 +273,7 @@ def tile_multilatentattention_pa_l_kernel(tc, x, w_down, w_up, out_k, out_v):
             if Q not in uc:
                 base = UC0 if Q == 0 else UCN + 22016 * (Q - 1)
                 uc[Q] = sb([P, 4, 1280], U32, base, "uc%d" % Q)
-                us[Q] = sb([P, 1280], U8, base + 20480, "us%d" % Q)
+                us[Q] = sb([P, 1280], U8, base + 20480 + 128, "us%d" % Q)
             nc.vector.quantize_mx(
                 out=uc[Q][:, G, c0:c0 + 4 * nf].bitcast(FP8),
                 scales=us[Q][4 * G:P, c0:c0 + 4 * nf],

@@ -16,357 +16,379 @@ ACT = mybir.ActivationFunctionType
 
 P = 128
 TWO_PI = 6.283185307179586
+ROPE_BASE = 10000.0
 
-XC = 0
-XS = 131072 + 128
-LC = 139648
-LS = 172608
-WC = 174720
-WS = 215872
-WR = 218432
-GR = 226624
-LB = 238912
-ID = 243008
-MISC = 243520
-XR = LC + 8192
-WR0 = XC + 3 * 32768
-GR0 = XC + 2 * 32768
-SRT = XC + 3 * 32768 + 16384
-SORT0 = 10
-SORT1 = 32
-UR = 0
-UC0 = 20480
-US0 = 40960
-COSF = 42496
-SINF = 50688
-TMP = 58880
-UCN = 65536
+HALF_QUADS = 32
+FIRST_BEAT = -2
+HEAD_BEATS = 32
+STAGE1_BEATS = 80
+SORT_FROM = 10
+
+KIB = 1024
+X_CODES = 0
+X_PLANES = X_CODES + 128 * KIB
+L_CODES = X_PLANES + 8 * KIB
+L_PLANES = L_CODES + 32 * KIB
+W_CODES = L_PLANES + 2 * KIB
+W_PLANES = W_CODES + 40 * KIB
+W_RAW = W_PLANES + 5 * 512
+GROUPED = W_RAW + 8 * KIB
+L_BF16 = GROUPED + 12 * KIB
+IDENTITY = L_BF16 + 4 * KIB
+WARM = IDENTITY + 512
+X_RAW = L_CODES + 8 * KIB
+W_RAW_LATE = L_CODES + 24 * KIB
+W_RAW_FIRST = X_CODES + 96 * KIB
+GROUPED_FIRST = X_CODES + 64 * KIB
+X_SORTED = X_CODES + 112 * KIB
+U_RAW = 0
+U_CODES_0 = 20 * KIB
+COS_TABLE = 41 * KIB + 512
+SIN_TABLE = COS_TABLE + 8 * KIB
+ROPE_TMP = SIN_TABLE + 8 * KIB
+U_CODES_1 = 64 * KIB
+U_CODES_STEP = 21 * KIB + 512
+
+ROPE, CONTENT, VALUE = (128, 64, 1024), (0, 128, 0), (192, 128, 512)
+
+
+def w_unit_beat(G, g):
+    quad, place = divmod(g, 4)
+    first = HEAD_BEATS + 16 * (G - 1)
+    if G == 0:
+        return 2 * quad - 2 + place // 2
+    if G == 1 and quad == 0:
+        return (11, 13, 19, 21)[place]
+    if G == 1:
+        return first - 4 + 2 * quad + place // 2
+    if quad == 0:
+        return first - 15 + 2 * place
+    return first - 6 + (10 * (g - 4)) // 12
 
 
 def tile_multilatentattention_pa_l_kernel(tc, x, w_down, w_up, out_k, out_v):
     nc = tc.nc
-    xf = x.flatten_outer_dims()
-    kf = out_k.rearrange("b s h d -> (b s) (h d)")
-    vf = out_v.rearrange("b s h d -> (b s) (h d)")
+    x_rows = x.flatten_outer_dims()
+    k_rows = out_k.rearrange("b s h d -> (b s) (h d)")
+    v_rows = out_v.rearrange("b s h d -> (b s) (h d)")
 
     with ExitStack() as ctx:
-        sbp = ctx.enter_context(tc.tile_pool(name="sb", bufs=1))
-        psp = ctx.enter_context(tc.psum_pool(name="ps", bufs=1))
+        sbuf_pool = ctx.enter_context(tc.tile_pool(name="sb", bufs=1))
+        psum_pool = ctx.enter_context(tc.psum_pool(name="ps", bufs=1))
         ctx.enter_context(tc.manual_schedule())
 
-        def sb(shape, dtype, off, tag):
-            return sbp.tile(shape, dtype, name=tag, tag=tag, offset=off, align_bytes=64)
+        def sb(shape, dtype, offset, tag):
+            return sbuf_pool.tile(shape, dtype, name=tag, tag=tag, offset=offset, align_bytes=64)
 
-        def bank(shape, k):
-            return psp.tile(shape, F32, name="b%d" % k, tag="b%d" % k)
+        def bank(shape, number):
+            return psum_pool.tile(shape, F32, name="b%d" % number, tag="b%d" % number)
 
-        def cp(eng, out, in_):
-            if eng == "V":
+        def copy(engine, out, in_):
+            if engine == "V":
                 nc.vector.tensor_copy(out=out, in_=in_)
             else:
                 nc.scalar.copy(out=out, in_=in_)
 
-        st = {"gr": 0, "lb": 0, "lq": 0}
-        xr, xq, tb, grx, xc, xs = {}, {}, {}, {}, {}, {}
-        wr, grw, wc, ws = {}, {}, {}, {}
-        acc, lbt, grl, lc, ls = {}, {}, {}, {}, {}
-        ur, uc, us = {}, {}, {}
+        count = {"grouped": 0, "l_bf16": 0, "l_quantised": 0}
+        x_raw, x_sorted, x_turned, x_grouped, x_codes, x_planes = {}, {}, {}, {}, {}, {}
+        w_raw, w_grouped, w_codes, w_planes = {}, {}, {}, {}
+        l_sums, l_bf16, l_grouped, l_codes, l_planes = {}, {}, {}, {}, {}
+        u_raw, u_codes, u_planes = {}, {}, {}
+        rope, out_sums = {}, {}
 
-        ident = sb([P, P], F32, ID, "ident")
-        make_identity(nc, ident[:])
-
-        chi = sb([P, 32], F32, MISC, "chi")
-        cmid = sb([P, 32], F32, MISC + 128, "cmid")
-        clo = sb([P, 32], F32, MISC + 256, "clo")
-        posi = sb([P, 8], I32, MISC + 384, "posi")
-        posf = sb([P, 8], F32, MISC + 448, "posf")
-        for i in range(32):
-            c = 10000.0 ** (-i / 32.0) / TWO_PI
-            hi = int(c * 65536.0) / 65536.0
-            mid = int((c - hi) * 1073741824.0) / 1073741824.0
-            lo = int((c - hi - mid) * 18014398509481984.0) / 18014398509481984.0
-            nc.gpsimd.memset(chi[:, i:i + 1], hi)
-            nc.gpsimd.memset(cmid[:, i:i + 1], mid)
-            nc.gpsimd.memset(clo[:, i:i + 1], lo)
-        nc.gpsimd.iota(posi[:], pattern=[[128, 8]], base=0, channel_multiplier=1)
-
-        FIRST = -2
-        LAST1 = 80
-
-        def need_w(G, a):
-            return 2 * a if G == 0 else 32 + 16 * (G - 1) + 2 * a
-
-        w_at = {}
-        for b in range(FIRST - 1, LAST1):
-            w_at[b] = []
+        w_units_of_beat = {}
+        for b in range(FIRST_BEAT, STAGE1_BEATS):
+            w_units_of_beat[b] = []
         for G in range(4):
             for g in range(16):
-                a, gl = divmod(g, 4)
-                if G == 0:
-                    e = 2 * a - 2 + gl // 2
-                elif a == 0:
-                    e = (10 + 4 * gl) if G == 1 else need_w(G, 0) - 15 + 2 * gl
-                elif G == 1:
-                    e = 30 + 2 * (a - 1) + gl // 2
-                else:
-                    e = need_w(G, 0) - 6 + (10 * (4 * (a - 1) + gl)) // 12
-                w_at[e].append((G, g))
-        order_w = []
-        for b in range(FIRST, LAST1):
-            order_w.extend(w_at[b])
+                w_units_of_beat[w_unit_beat(G, g)].append((G, g))
+        w_order = []
+        for b in range(FIRST_BEAT, STAGE1_BEATS):
+            w_order.extend(w_units_of_beat[b])
 
-        def new_gr(b):
-            k = st["gr"]
-            st["gr"] = k + 1
+        def new_grouped(b):
+            turn = count["grouped"]
+            count["grouped"] = turn + 1
             if b < 8:
-                return sb([P, 2048], BF16, GR0 + 4096 * (k % 8), "gra%d" % (k % 8))
-            n = 3 if b < 32 else 2
-            return sb([P, 2048], BF16, GR + 4096 * (k % n), "gr%d" % (k % n))
+                return sb([P, 2048], BF16, GROUPED_FIRST + 4 * KIB * (turn % 8), "gra%d" % (turn % 8))
+            slots = 3 if b < HEAD_BEATS else 2
+            return sb([P, 2048], BF16, GROUPED + 4 * KIB * (turn % slots), "gr%d" % (turn % slots))
 
         def load_x(n):
-            c, hq = divmod(n, 8)
-            t = sb([P, 4, 1024], BF16, XR + 8192 * (n % 3), "xr%d" % (n % 3))
-            src = xf[512 * c:512 * (c + 1), 1024 * hq:1024 * (hq + 1)].rearrange("(i p) k -> p i k", p=P)
+            chunk, part = divmod(n, 8)
+            raw = sb([P, 4, 1024], BF16, X_RAW + 8 * KIB * (n % 3), "xr%d" % (n % 3))
+            rows = x_rows[512 * chunk:512 * (chunk + 1), 1024 * part:1024 * (part + 1)]
+            rows = rows.rearrange("(i p) k -> p i k", p=P)
             if n == 0:
-                for i in range(4):
-                    nc.sync.dma_start(out=t[:, i, :], in_=src[:, i, :])
+                for token_tile in range(4):
+                    nc.sync.dma_start(out=raw[:, token_tile, :], in_=rows[:, token_tile, :])
             else:
-                nc.sync.dma_start(out=t[:], in_=src)
-            xr[n] = t
+                nc.sync.dma_start(out=raw[:], in_=rows)
+            x_raw[n] = raw
 
-        def sort_x(n, eng):
+        def sort_x(n):
             if n < 30:
-                t = sb([P, 8, 2, 128], F32, SRT + 8192 * (n % 2), "xq%d" % (n % 2))
+                ordered = sb([P, 8, 2, P], F32, X_SORTED + 8 * KIB * (n % 2), "xq%d" % (n % 2))
             else:
-                t = sb([P, 8, 2, 128], F32, WC + 8192 * (n - 30), "xq%d" % (n - 28))
-            cp(eng, t[:], xr[n][:].rearrange("p i k -> p (i k)").bitcast(F32).rearrange("p (q w u) -> p q u w", u=2, w=128))
-            xq[n] = t
+                ordered = sb([P, 8, 2, P], F32, W_CODES + 8 * KIB * (n - 30), "xq%d" % (n - 28))
+            words = x_raw[n][:].rearrange("p i k -> p (i k)").bitcast(F32)
+            nc.vector.tensor_copy(out=ordered[:], in_=words.rearrange("p (q w u) -> p q u w", u=2, w=P))
+            x_sorted[n] = ordered
 
-        def transposes(n):
-            for g2 in range(2):
-                for hb in range(2):
-                    t = bank([P, 2, 256], 4 + 2 * g2 + hb)
-                    for i2 in range(2):
-                        words = xr[n][:, 2 * hb + i2, :].bitcast(F32)
+        def transpose_x(n):
+            for o in range(2):
+                for half in range(2):
+                    turned = bank([P, 2, 256], 4 + 2 * o + half)
+                    for side in range(2):
+                        token_tile = 2 * half + side
                         for u in range(2):
-                            if n in xq:
-                                src = xq[n][:, 2 * (2 * hb + i2) + g2, u, :]
+                            if n in x_sorted:
+                                words = x_sorted[n][:, 2 * token_tile + o, u, :]
                             else:
-                                src = words[:, 256 * g2 + u:256 * (g2 + 1):2]
-                            nc.tensor.transpose(t[:, u, 128 * i2:128 * (i2 + 1)], src, ident[:])
-                    tb[(n, g2, hb)] = t
+                                words = x_raw[n][:, token_tile, :].bitcast(F32)[:, 256 * o + u:256 * (o + 1):2]
+                            nc.tensor.transpose(turned[:, u, P * side:P * (side + 1)], words, identity[:])
+                    x_turned[(n, o, half)] = turned
 
-        def copy_x(n, g2, hb, eng, b):
-            if (n, g2) not in grx:
-                grx[(n, g2)] = new_gr(b)
-            gw = grx[(n, g2)][:].bitcast(F32).rearrange("p (r u) -> p r u", u=2)
-            cp(eng, gw[:, 256 * hb:256 * (hb + 1), :], tb[(n, g2, hb)][:].rearrange("p u r -> p r u"))
+        def copy_x(n, o, half, engine, b):
+            if (n, o) not in x_grouped:
+                x_grouped[(n, o)] = new_grouped(b)
+            words = x_grouped[(n, o)][:].bitcast(F32).rearrange("p (r u) -> p r u", u=2)
+            copy(engine, words[:, 256 * half:256 * (half + 1), :], x_turned[(n, o, half)][:].rearrange("p u r -> p r u"))
 
-        def quant_x(n, g2):
-            c, hq = divmod(n, 8)
-            a, h = divmod(hq, 2)
-            gl = 2 * h + g2
-            if (c, a) not in xc:
-                xc[(c, a)] = sb([P, 4, 512], U32, XC + 8192 * (4 * c + a), "xc%d" % (4 * c + a))
-                xs[(c, a)] = sb([P, 512], U8, XS + 512 * (4 * c + a), "xs%d" % (4 * c + a))
+        def quantise_x(n, o):
+            chunk, part = divmod(n, 8)
+            quad, later = divmod(part, 2)
+            place = 2 * later + o
+            if (chunk, quad) not in x_codes:
+                number = 4 * chunk + quad
+                x_codes[(chunk, quad)] = sb([P, 4, 512], U32, X_CODES + 8 * KIB * number, "xc%d" % number)
+                x_planes[(chunk, quad)] = sb([P, 512], U8, X_PLANES + 512 * number, "xs%d" % number)
             nc.vector.quantize_mx(
-                out=xc[(c, a)][:, gl, :].bitcast(FP8), scales=xs[(c, a)][4 * gl:P, :], in_=grx[(n, g2)][:]
+                out=x_codes[(chunk, quad)][:, place, :].bitcast(FP8),
+                scales=x_planes[(chunk, quad)][4 * place:P, :],
+                in_=x_grouped[(n, o)][:],
             )
 
-        def load_w(k):
-            G, g = order_w[k]
+        def load_w(number):
+            G, g = w_order[number]
             if G == 0:
-                t = sb([P, 4, 512], BF16, WR0 + 4096 * (k % 8), "wra%d" % (k % 8))
-            elif k < 20:
-                t = sb([P, 4, 512], BF16, WR + 4096 * (k % 2), "wr%d" % (k % 2))
+                raw = sb([P, 4, 512], BF16, W_RAW_FIRST + 4 * KIB * (number % 8), "wra%d" % (number % 8))
+            elif number < 20:
+                raw = sb([P, 4, 512], BF16, W_RAW + 4 * KIB * (number % 2), "wr%d" % (number % 2))
             else:
-                t = sb([P, 4, 512], BF16, (WR, WR + 4096, LC + 24576, LC + 28672)[k % 4], "wr%d" % (k % 4))
-            nc.sync.dma_start(
-                out=t[:],
-                in_=w_down[512 * g:512 * (g + 1), 512 * G:512 * (G + 1)].rearrange("(p j) c -> p j c", j=4),
-            )
-            wr[(G, g)] = t
+                offset = (W_RAW, W_RAW + 4 * KIB, W_RAW_LATE, W_RAW_LATE + 4 * KIB)[number % 4]
+                raw = sb([P, 4, 512], BF16, offset, "wr%d" % (number % 4))
+            rows = w_down[512 * g:512 * (g + 1), 512 * G:512 * (G + 1)]
+            nc.sync.dma_start(out=raw[:], in_=rows.rearrange("(p j) c -> p j c", j=4))
+            w_raw[(G, g)] = raw
 
-        def inter_w(G, g, eng, b):
-            t = new_gr(b)
-            grw[(G, g)] = t
-            cp(
-                eng,
-                t[:].rearrange("p (t m j) -> p t m j", t=4, j=4),
-                wr[(G, g)][:].rearrange("p j (m t) -> p t m j", t=4),
+        def interleave_w(G, g, engine, b):
+            grouped = new_grouped(b)
+            w_grouped[(G, g)] = grouped
+            copy(
+                engine,
+                grouped[:].rearrange("p (t m j) -> p t m j", t=4, j=4),
+                w_raw[(G, g)][:].rearrange("p j (m t) -> p t m j", t=4),
             )
-            k = order_w.index((G, g))
-            if k < 10:
-                load_w(k + 6)
-            elif 14 <= k < 18:
-                load_w(k + 2)
-            elif 20 <= k < 60:
-                load_w(k + 4)
+            number = w_order.index((G, g))
+            if number < 10:
+                load_w(number + 6)
+            elif 14 <= number < 18:
+                load_w(number + 2)
+            elif 20 <= number < 60:
+                load_w(number + 4)
 
-        def quant_w(G, g):
-            a, gl = divmod(g, 4)
-            if (G, a) not in wc:
-                s = (4 * G + a) % 5
-                wc[(G, a)] = sb([P, 4, 512], U32, WC + 8192 * s, "wc%d" % s)
-                ws[(G, a)] = sb([P, 512], U8, WS + 512 * s, "ws%d" % s)
+        def quantise_w(G, g):
+            quad, place = divmod(g, 4)
+            if (G, quad) not in w_codes:
+                slot = (4 * G + quad) % 5
+                w_codes[(G, quad)] = sb([P, 4, 512], U32, W_CODES + 8 * KIB * slot, "wc%d" % slot)
+                w_planes[(G, quad)] = sb([P, 512], U8, W_PLANES + 512 * slot, "ws%d" % slot)
             nc.vector.quantize_mx(
-                out=wc[(G, a)][:, gl, :].bitcast(FP8), scales=ws[(G, a)][4 * gl:P, :], in_=grw[(G, g)][:]
+                out=w_codes[(G, quad)][:, place, :].bitcast(FP8),
+                scales=w_planes[(G, quad)][4 * place:P, :],
+                in_=w_grouped[(G, g)][:],
             )
 
-        def mm1(G, c, a, t, k):
-            if a == 0:
-                acc[(G, c, t)] = bank([P, 512], k)
-            for gl in range(4):
+        def multiply_1(G, chunk, quad, t, bank_number):
+            if quad == 0:
+                l_sums[(G, chunk, t)] = bank([P, 512], bank_number)
+            for place in range(4):
                 nc.tensor.matmul_mx(
-                    out=acc[(G, c, t)][:],
-                    lhsT=wc[(G, a)][:, gl, 128 * t:128 * (t + 1)].bitcast(FP8),
-                    lhsT_scale=ws[(G, a)][4 * gl:P, 128 * t:128 * (t + 1)],
-                    rhs=xc[(c, a)][:, gl, :].bitcast(FP8),
-                    rhs_scale=xs[(c, a)][4 * gl:P, :],
-                    start=(a == 0 and gl == 0),
-                    stop=(a == 3 and gl == 3),
+                    out=l_sums[(G, chunk, t)][:],
+                    lhsT=w_codes[(G, quad)][:, place, P * t:P * (t + 1)].bitcast(FP8),
+                    lhsT_scale=w_planes[(G, quad)][4 * place:P, P * t:P * (t + 1)],
+                    rhs=x_codes[(chunk, quad)][:, place, :].bitcast(FP8),
+                    rhs_scale=x_planes[(chunk, quad)][4 * place:P, :],
+                    start=(quad == 0 and place == 0),
+                    stop=(quad == 3 and place == 3),
                 )
 
-        def evac_lat(G, c, t, eng, b):
-            if (G, c) not in lbt:
-                k = st["lb"]
-                st["lb"] = k + 1
-                if b < 32 or k % 2 == 0:
-                    lbt[(G, c)] = sb([P, 4, 512], BF16, LB, "lb0")
+        def round_latent(G, chunk, t, b):
+            if (G, chunk) not in l_bf16:
+                turn = count["l_bf16"]
+                count["l_bf16"] = turn + 1
+                if b < HEAD_BEATS or turn % 2 == 0:
+                    l_bf16[(G, chunk)] = sb([P, 4, 512], BF16, L_BF16, "lb0")
                 else:
-                    lbt[(G, c)] = sb([P, 4, 512], BF16, GR + 8192, "lb1")
-            cp(eng, lbt[(G, c)][:, t, :], acc[(G, c, t)][:])
+                    l_bf16[(G, chunk)] = sb([P, 4, 512], BF16, GROUPED + 8 * KIB, "lb1")
+            nc.scalar.copy(out=l_bf16[(G, chunk)][:, t, :], in_=l_sums[(G, chunk, t)][:])
 
-        def inter_lat(G, c, b):
-            t = new_gr(b)
-            grl[(G, c)] = t
+        latent_waiting = []
+
+        def interleave_latent(G, chunk, b):
+            grouped = new_grouped(b)
+            l_grouped[(G, chunk)] = grouped
             nc.vector.tensor_copy(
-                out=t[:].rearrange("p (r t) -> p r t", t=4), in_=lbt[(G, c)][:].rearrange("p t r -> p r t")
+                out=grouped[:].rearrange("p (r t) -> p r t", t=4), in_=l_bf16[(G, chunk)][:].rearrange("p t r -> p r t")
             )
+            latent_waiting.append((G, chunk))
 
-        def quant_lat(G, c):
-            lc[(G, c)] = sb([P, 512], U32, LC + 2048 * (4 * G + c), "lc%d" % (4 * G + c))
-            if c not in ls:
-                ls[c] = sb([P, 512], U8, LS + 512 * c, "ls%d" % c)
-            nc.vector.quantize_mx(out=lc[(G, c)][:].bitcast(FP8), scales=ls[c][4 * G:P, :], in_=grl[(G, c)][:])
+        def quantise_latent():
+            done = count["l_quantised"]
+            if done < len(latent_waiting):
+                G, chunk = latent_waiting[done]
+                count["l_quantised"] = done + 1
+                number = 4 * G + chunk
+                l_codes[(G, chunk)] = sb([P, 512], U32, L_CODES + 2 * KIB * number, "lc%d" % number)
+                if chunk not in l_planes:
+                    l_planes[chunk] = sb([P, 512], U8, L_PLANES + 512 * chunk, "ls%d" % chunk)
+                nc.vector.quantize_mx(
+                    out=l_codes[(G, chunk)][:].bitcast(FP8), scales=l_planes[chunk][4 * G:P, :], in_=l_grouped[(G, chunk)][:]
+                )
 
-        def load_u(k):
-            Q, G = divmod(k, 4)
-            t = sb([P, 4, 1280], BF16, UR + 10240 * (k % 2), "ur%d" % (k % 2))
-            nc.sync.dma_start(
-                out=t[:],
-                in_=w_up[512 * G:512 * (G + 1), 1280 * Q:1280 * (Q + 1)].rearrange("(p j) c -> p j c", j=4),
-            )
-            ur[(Q, G)] = t
+        def load_u(number):
+            Q, G = divmod(number, 4)
+            raw = sb([P, 4, 1280], BF16, U_RAW + 10 * KIB * (number % 2), "ur%d" % (number % 2))
+            rows = w_up[512 * G:512 * (G + 1), 1280 * Q:1280 * (Q + 1)]
+            nc.sync.dma_start(out=raw[:], in_=rows.rearrange("(p t) c -> p t c", t=4))
+            u_raw[(Q, G)] = raw
 
-        PARTS = ((0, 128, 0), (192, 128, 512), (128, 64, 1024))
+        def interleave_u(Q, G, part, engine, b):
+            feature, features = part[0], part[1]
+            grouped = new_grouped(b)
+            columns = u_raw[(Q, G)][:].rearrange("p t (h w) -> p h w t", h=4)[:, :, feature:feature + features, :]
+            copy(engine, grouped[:, 0:16 * features].rearrange("p (h m t) -> p h m t", h=4, t=4), columns)
+            return grouped
 
-        def prep_u(Q, G, part, eng, b):
-            f0, nf, c0 = PARTS[part]
-            t = new_gr(b)
-            src = ur[(Q, G)][:].rearrange("p j (h w) -> p h w j", h=4)[:, :, f0:f0 + nf, :]
-            cp(eng, t[:, 0:16 * nf].rearrange("p (h m j) -> p h m j", h=4, j=4), src)
-            return t
-
-        def quant_u(Q, G, part, t):
-            f0, nf, c0 = PARTS[part]
-            if Q not in uc:
-                base = UC0 if Q == 0 else UCN + 22016 * (Q - 1)
-                uc[Q] = sb([P, 4, 1280], U32, base, "uc%d" % Q)
-                us[Q] = sb([P, 1280], U8, base + 20480 + 128, "us%d" % Q)
+        def quantise_u(Q, G, part, grouped):
+            features, column = part[1], part[2]
+            if Q not in u_codes:
+                offset = U_CODES_0 if Q == 0 else U_CODES_1 + U_CODES_STEP * (Q - 1)
+                u_codes[Q] = sb([P, 4, 1280], U32, offset, "uc%d" % Q)
+                u_planes[Q] = sb([P, 1280], U8, offset + 20 * KIB, "us%d" % Q)
             nc.vector.quantize_mx(
-                out=uc[Q][:, G, c0:c0 + 4 * nf].bitcast(FP8),
-                scales=us[Q][4 * G:P, c0:c0 + 4 * nf],
-                in_=t[:, 0:16 * nf],
+                out=u_codes[Q][:, G, column:column + 4 * features].bitcast(FP8),
+                scales=u_planes[Q][4 * G:P, column:column + 4 * features],
+                in_=grouped[:, 0:16 * features],
             )
 
-        def unit_u(Q, G, b):
-            t0 = prep_u(Q, G, 0, "V", b)
-            t1 = prep_u(Q, G, 1, "S", b)
-            quant_u(Q, G, 0, t0)
-            t2 = prep_u(Q, G, 2, "V", b)
+        def prepare_u(Q, G, b):
+            content = interleave_u(Q, G, CONTENT, "V", b)
+            value = interleave_u(Q, G, VALUE, "S", b)
+            quantise_u(Q, G, CONTENT, content)
+            rotary = interleave_u(Q, G, ROPE, "V", b)
             if 4 * Q + G + 2 < 16:
                 load_u(4 * Q + G + 2)
-            quant_u(Q, G, 1, t1)
-            quant_u(Q, G, 2, t2)
+            quantise_u(Q, G, VALUE, value)
+            quantise_u(Q, G, ROPE, rotary)
 
-        rope = {}
+        def rope_constants():
+            rope["chi"] = sb([P, 32], F32, IDENTITY, "chi")
+            rope["cmid"] = sb([P, 32], F32, IDENTITY + 128, "cmid")
+            rope["clo"] = sb([P, 32], F32, IDENTITY + 256, "clo")
+            rope["posi"] = sb([P, 8], I32, IDENTITY + 384, "posi")
+            rope["posf"] = sb([P, 8], F32, IDENTITY + 448, "posf")
+            for frequency in range(32):
+                turns = ROPE_BASE ** (-frequency / 32.0) / TWO_PI
+                high = int(turns * 2.0 ** 16) / 2.0 ** 16
+                middle = int((turns - high) * 2.0 ** 30) / 2.0 ** 30
+                low = int((turns - high - middle) * 2.0 ** 54) / 2.0 ** 54
+                column = slice(frequency, frequency + 1)
+                nc.gpsimd.memset(rope["chi"][:, column], high)
+                nc.gpsimd.memset(rope["cmid"][:, column], middle)
+                nc.gpsimd.memset(rope["clo"][:, column], low)
+            nc.gpsimd.iota(rope["posi"][:], pattern=[[P, 8]], base=0, channel_multiplier=1)
 
         def rope_tables():
-            nc.vector.tensor_copy(out=posf[:], in_=posi[:])
-            tm = [sb([P, 8, 32], F32, TMP + 1024 * k, "tmp%d" % k) for k in range(5)]
-            ti = sb([P, 8, 32], I32, TMP + 1024 * 5, "tmpi")
+            position = rope["posf"]
+            nc.vector.tensor_copy(out=position[:], in_=rope["posi"][:])
+            tmp = [sb([P, 8, 32], F32, ROPE_TMP + KIB * number, "tmp%d" % number) for number in range(5)]
+            whole = sb([P, 8, 32], I32, ROPE_TMP + KIB * 5, "tmpi")
             for s in range(8):
-                nc.vector.tensor_scalar_mul(out=tm[0][:, s, :], in0=chi[:], scalar1=posf[:, s:s + 1])
-                nc.vector.tensor_scalar_mul(out=tm[1][:, s, :], in0=cmid[:], scalar1=posf[:, s:s + 1])
-                nc.vector.tensor_scalar_mul(out=tm[2][:, s, :], in0=clo[:], scalar1=posf[:, s:s + 1])
-            nc.vector.tensor_copy(out=ti[:], in_=tm[0][:])
-            nc.vector.tensor_copy(out=tm[3][:], in_=ti[:])
-            nc.vector.tensor_tensor(out=tm[0][:], in0=tm[0][:], in1=tm[3][:], op=ALU.subtract)
-            nc.vector.tensor_tensor(out=tm[1][:], in0=tm[1][:], in1=tm[2][:], op=ALU.add)
-            nc.vector.tensor_tensor(out=tm[0][:], in0=tm[0][:], in1=tm[1][:], op=ALU.add)
-            nc.vector.tensor_scalar_add(out=tm[1][:], in0=tm[0][:], scalar1=0.25)
-            nc.vector.scalar_tensor_tensor(out=tm[2][:], in0=tm[0][:], scalar=0.5, in1=tm[0][:], op0=ALU.is_gt, op1=ALU.subtract)
-            nc.vector.scalar_tensor_tensor(out=tm[3][:], in0=tm[1][:], scalar=0.5, in1=tm[1][:], op0=ALU.is_gt, op1=ALU.subtract)
-            nc.scalar.activation(out=tm[0][:], in_=tm[2][:], func=ACT.Sin, scale=-TWO_PI)
-            nc.scalar.activation(out=tm[1][:], in_=tm[2][:], func=ACT.Sin, scale=TWO_PI)
-            nc.scalar.activation(out=tm[4][:], in_=tm[3][:], func=ACT.Sin, scale=-TWO_PI)
-            cosf = sb([P, 8, 8, 32], F32, COSF, "cosf")
-            sinf = sb([P, 8, 8, 32], F32, SINF, "sinf")
-            for hh in range(8):
-                nc.vector.tensor_copy(out=cosf[:, :, hh, :], in_=tm[4][:])
-                nc.vector.tensor_copy(out=sinf[:, :, hh, :], in_=tm[1 - hh % 2][:])
-            rope["cos"] = cosf
-            rope["sin"] = sinf
+                nc.vector.tensor_scalar_mul(out=tmp[0][:, s, :], in0=rope["chi"][:], scalar1=position[:, s:s + 1])
+                nc.vector.tensor_scalar_mul(out=tmp[1][:, s, :], in0=rope["cmid"][:], scalar1=position[:, s:s + 1])
+                nc.vector.tensor_scalar_mul(out=tmp[2][:, s, :], in0=rope["clo"][:], scalar1=position[:, s:s + 1])
+            nc.vector.tensor_copy(out=whole[:], in_=tmp[0][:])
+            nc.vector.tensor_copy(out=tmp[3][:], in_=whole[:])
+            nc.vector.tensor_tensor(out=tmp[0][:], in0=tmp[0][:], in1=tmp[3][:], op=ALU.subtract)
+            nc.vector.tensor_tensor(out=tmp[1][:], in0=tmp[1][:], in1=tmp[2][:], op=ALU.add)
+            nc.vector.tensor_tensor(out=tmp[0][:], in0=tmp[0][:], in1=tmp[1][:], op=ALU.add)
+            nc.vector.tensor_scalar_add(out=tmp[1][:], in0=tmp[0][:], scalar1=0.25)
+            nc.vector.scalar_tensor_tensor(
+                out=tmp[2][:], in0=tmp[0][:], scalar=0.5, in1=tmp[0][:], op0=ALU.is_gt, op1=ALU.subtract
+            )
+            nc.vector.scalar_tensor_tensor(
+                out=tmp[3][:], in0=tmp[1][:], scalar=0.5, in1=tmp[1][:], op0=ALU.is_gt, op1=ALU.subtract
+            )
+            nc.scalar.activation(out=tmp[0][:], in_=tmp[2][:], func=ACT.Sin, scale=-TWO_PI)
+            nc.scalar.activation(out=tmp[1][:], in_=tmp[2][:], func=ACT.Sin, scale=TWO_PI)
+            nc.scalar.activation(out=tmp[4][:], in_=tmp[3][:], func=ACT.Sin, scale=-TWO_PI)
+            rope["cos"] = sb([P, 8, 8, 32], F32, COS_TABLE, "cosf")
+            rope["sin"] = sb([P, 8, 8, 32], F32, SIN_TABLE, "sinf")
+            for head_half in range(8):
+                nc.vector.tensor_copy(out=rope["cos"][:, :, head_half, :], in_=tmp[4][:])
+                nc.vector.tensor_copy(out=rope["sin"][:, :, head_half, :], in_=tmp[1 - head_half % 2][:])
 
-        ot = {}
-
-        def mm2(Q, i):
-            s = 16 * Q + i
-            c, il = divmod(i, 4)
-            tiles = []
-            for k, part in enumerate((2, 0, 1)):
-                f0, nf, c0 = PARTS[part]
-                t = bank([P, 4 * nf], (3 * s + k + 4) % 8)
+        def multiply_2(step):
+            Q, token_tile = divmod(step, 16)
+            chunk, side = divmod(token_tile, 4)
+            sums = []
+            for number, part in enumerate((ROPE, CONTENT, VALUE)):
+                features, column = part[1], part[2]
+                acc = bank([P, 4 * features], (3 * step + number + 4) % 8)
                 for G in range(4):
                     nc.tensor.matmul_mx(
-                        out=t[:],
-                        lhsT=lc[(G, c)][:, 128 * il:128 * (il + 1)].bitcast(FP8),
-                        lhsT_scale=ls[c][4 * G:P, 128 * il:128 * (il + 1)],
-                        rhs=uc[Q][:, G, c0:c0 + 4 * nf].bitcast(FP8),
-                        rhs_scale=us[Q][4 * G:P, c0:c0 + 4 * nf],
+                        out=acc[:],
+                        lhsT=l_codes[(G, chunk)][:, P * side:P * (side + 1)].bitcast(FP8),
+                        lhsT_scale=l_planes[chunk][4 * G:P, P * side:P * (side + 1)],
+                        rhs=u_codes[Q][:, G, column:column + 4 * features].bitcast(FP8),
+                        rhs_scale=u_planes[Q][4 * G:P, column:column + 4 * features],
                         start=(G == 0),
                         stop=(G == 3),
                     )
-                tiles.append(t)
-            ot[s] = tiles
+                sums.append(acc)
+            out_sums[step] = sums
 
-        def evac2(Q, i):
-            s = 16 * Q + i
-            pr, pc, pv = ot[s]
-            base = WC + 8192 * (1 + s % 4)
-            okt = sb([P, 4, 192], F32, base, "ok%d" % (s % 4))
-            ovt = sb([P, 512], F32, base + 3072, "ov%d" % (s % 4))
-            t1 = sb([P, 4, 2, 32], F32, base + 5120, "ta%d" % (s % 4))
-            t2 = sb([P, 4, 2, 32], F32, base + 6144, "tb%d" % (s % 4))
-            nc.scalar.copy(out=okt[:, :, 0:128], in_=pc[:].rearrange("p (h m) -> p h m", h=4))
-            nc.scalar.copy(out=ovt[:], in_=pv[:])
-            prv = pr[:].rearrange("p (h e r) -> p h e r", h=4, e=2)
-            cosv = rope["cos"][:, i % 8, :, :].rearrange("p (h e) r -> p h e r", e=2)
-            sinv = rope["sin"][:, i % 8, :, :].rearrange("p (h e) r -> p h e r", e=2)
-            nc.vector.tensor_tensor(out=t1[:], in0=prv, in1=cosv, op=ALU.mult)
-            nc.vector.tensor_tensor(out=t2[:, :, 0, :], in0=prv[:, :, 1, :], in1=sinv[:, :, 0, :], op=ALU.mult)
-            nc.vector.tensor_tensor(out=t2[:, :, 1, :], in0=prv[:, :, 0, :], in1=sinv[:, :, 1, :], op=ALU.mult)
+        def store_2(step):
+            Q, token_tile = divmod(step, 16)
+            rotary, content, value = out_sums[step]
+            slot = step % 4
+            offset = W_CODES + 8 * KIB * (1 + slot)
+            k_tile = sb([P, 4, 192], F32, offset, "ok%d" % slot)
+            v_tile = sb([P, 512], F32, offset + 3 * KIB, "ov%d" % slot)
+            straight = sb([P, 4, 2, 32], F32, offset + 5 * KIB, "ta%d" % slot)
+            crossed = sb([P, 4, 2, 32], F32, offset + 6 * KIB, "tb%d" % slot)
+            nc.scalar.copy(out=k_tile[:, :, 0:128], in_=content[:].rearrange("p (h m) -> p h m", h=4))
+            nc.scalar.copy(out=v_tile[:], in_=value[:])
+            u = rotary[:].rearrange("p (h e r) -> p h e r", h=4, e=2)
+            cos = rope["cos"][:, token_tile % 8, :, :].rearrange("p (h e) r -> p h e r", e=2)
+            sin = rope["sin"][:, token_tile % 8, :, :].rearrange("p (h e) r -> p h e r", e=2)
+            nc.vector.tensor_tensor(out=straight[:], in0=u, in1=cos, op=ALU.mult)
+            nc.vector.tensor_tensor(out=crossed[:, :, 0, :], in0=u[:, :, 1, :], in1=sin[:, :, 0, :], op=ALU.mult)
+            nc.vector.tensor_tensor(out=crossed[:, :, 1, :], in0=u[:, :, 0, :], in1=sin[:, :, 1, :], op=ALU.mult)
             nc.vector.tensor_tensor(
-                out=okt[:, :, 128:192],
-                in0=t1[:].rearrange("p h e r -> p h (e r)"),
-                in1=t2[:].rearrange("p h e r -> p h (e r)"),
+                out=k_tile[:, :, 128:192],
+                in0=straight[:].rearrange("p h e r -> p h (e r)"),
+                in1=crossed[:].rearrange("p h e r -> p h (e r)"),
                 op=ALU.add,
             )
-            nc.sync.dma_start(out=vf[128 * i:128 * (i + 1), 512 * Q:512 * (Q + 1)], in_=ovt[:])
-            nc.sync.dma_start(
-                out=kf[128 * i:128 * (i + 1), 768 * Q:768 * (Q + 1)], in_=okt[:].rearrange("p h d -> p (h d)")
-            )
+            tokens = slice(P * token_tile, P * (token_tile + 1))
+            nc.sync.dma_start(out=v_rows[tokens, 512 * Q:512 * (Q + 1)], in_=v_tile[:])
+            nc.sync.dma_start(out=k_rows[tokens, 768 * Q:768 * (Q + 1)], in_=k_tile[:].rearrange("p h d -> p (h d)"))
+
+        identity = sb([P, P], F32, IDENTITY, "ident")
+        make_identity(nc, identity[:])
 
         load_x(0)
         load_w(0)
@@ -378,101 +400,92 @@ def tile_multilatentattention_pa_l_kernel(tc, x, w_down, w_up, out_k, out_v):
         load_w(4)
         load_w(5)
 
-        nc.vector.memset(posf[:], 0.0)
-        nc.scalar.copy(out=posf[:], in_=posf[:])
+        warm = sb([P, 8], F32, WARM, "warm")
+        nc.vector.memset(warm[:], 0.0)
+        nc.scalar.copy(out=warm[:], in_=warm[:])
 
-        pend_q = []
+        for b in range(FIRST_BEAT, STAGE1_BEATS):
+            head = b < HEAD_BEATS
+            turning = b + 2 < HALF_QUADS
+            units = w_units_of_beat[b]
 
-        def flush_lat():
-            k = st["lq"]
-            if k < len(pend_q):
-                quant_lat(pend_q[k][0], pend_q[k][1])
-                st["lq"] = k + 1
+            if turning:
+                transpose_x(b + 2)
+            if 0 <= b < HEAD_BEATS:
+                G = 0
+                chunk, rest = divmod(b, 8)
+                quad, half = divmod(rest, 2)
+                channel_tiles = (2 * half, 2 * half + 1)
+                for t in channel_tiles:
+                    multiply_1(G, chunk, quad, t, t)
+            elif b >= HEAD_BEATS:
+                G, rest = divmod(b - HEAD_BEATS, 16)
+                G = G + 1
+                pair, rest = divmod(rest, 8)
+                quad, second = divmod(rest, 2)
+                chunk = 2 * pair + second
+                channel_tiles = (0, 1, 2, 3)
+                for t in channel_tiles:
+                    multiply_1(G, chunk, quad, t, 4 * (1 - second) + t)
 
-        for b in range(FIRST, LAST1):
-            head = b < 32
-            units = w_at[b]
-            n = b + 2
-            if head and n < 32:
-                transposes(n)
-            if b >= 0:
-                if head:
-                    c, r = divmod(b, 8)
-                    a, half = divmod(r, 2)
-                    for t in (2 * half, 2 * half + 1):
-                        mm1(0, c, a, t, t)
-                else:
-                    G, r = divmod(b - 32, 16)
-                    G = G + 1
-                    hs, r = divmod(r, 8)
-                    a, cl = divmod(r, 2)
-                    c = 2 * hs + cl
-                    for t in range(4):
-                        mm1(G, c, a, t, 4 * (1 - cl) + t)
-            if head and b + 5 < 32:
+            if b + 5 < HALF_QUADS:
                 load_x(b + 5)
-            if SORT0 <= b + 3 < SORT1:
-                sort_x(b + 3, "S")
-            if head and n < 32:
-                copy_x(n, 0, 0, "V" if b < 8 else "S", b)
-                copy_x(n, 0, 1, "S" if b < 8 else "V", b)
-                copy_x(n, 1, 0, "S", b)
-                copy_x(n, 1, 1, "S" if b < 8 else "V", b)
-                quant_x(n, 0)
+            if SORT_FROM <= b + 3 < HALF_QUADS:
+                sort_x(b + 3)
+            if turning:
+                copy_x(b + 2, 0, 0, "V" if b < 8 else "S", b)
+                copy_x(b + 2, 0, 1, "S", b)
+                copy_x(b + 2, 1, 0, "S", b)
+                copy_x(b + 2, 1, 1, "S", b)
+                quantise_x(b + 2, 0)
             else:
-                flush_lat()
-            for k, (wG, wg) in enumerate(units):
+                quantise_latent()
+
+            for number, (unit_G, unit_g) in enumerate(units):
                 if head:
-                    eng = "S" if (k == 0 and not SORT0 <= b + 3 < SORT1) else "V"
+                    engine = "S" if number == 0 else "V"
                 else:
-                    eng = "S" if (wg % 2 == 0) else "V"
-                inter_w(wG, wg, eng, b)
-                if k == 0:
-                    flush_lat()
-                    if head and n < 32:
-                        quant_x(n, 1)
+                    engine = "S" if unit_g % 2 == 0 else "V"
+                interleave_w(unit_G, unit_g, engine, b)
+                if number == 0:
+                    quantise_latent()
+                    if turning:
+                        quantise_x(b + 2, 1)
                 else:
-                    quant_w(units[k - 1][0], units[k - 1][1])
+                    quantise_w(units[number - 1][0], units[number - 1][1])
             if units:
-                quant_w(units[-1][0], units[-1][1])
+                quantise_w(units[-1][0], units[-1][1])
             else:
-                flush_lat()
-                if head and n < 32:
-                    quant_x(n, 1)
-            if b >= 0:
-                if head:
-                    if a == 3:
-                        for t in (2 * half, 2 * half + 1):
-                            evac_lat(0, c, t, "V" if SORT0 <= b + 3 < SORT1 else "S", b)
-                        if half == 1:
-                            inter_lat(0, c, b)
-                            pend_q.append((0, c))
-                else:
-                    if a == 3:
-                        for t in range(4):
-                            evac_lat(G, c, t, "S", b)
-                        inter_lat(G, c, b)
-                        pend_q.append((G, c))
+                quantise_latent()
+                if turning:
+                    quantise_x(b + 2, 1)
+
+            if b >= 0 and quad == 3:
+                for t in channel_tiles:
+                    round_latent(G, chunk, t, b)
+                if not head:
+                    interleave_latent(G, chunk, b)
+            if 8 <= b <= HEAD_BEATS and b % 8 == 0:
+                interleave_latent(0, b // 8 - 1, b)
+
             if b == 27:
-                for k in range(20, 24):
-                    load_w(k)
+                for number in range(20, 24):
+                    load_w(number)
+            if b == 30:
+                rope_constants()
             if b == 71:
                 load_u(0)
                 load_u(1)
             if b == 72:
                 rope_tables()
             if b in (73, 74, 76, 77):
-                G2 = (73, 74, 76, 77).index(b)
-                unit_u(0, G2, b)
-        flush_lat()
-        flush_lat()
+                prepare_u(0, (73, 74, 76, 77).index(b), b)
+        quantise_latent()
 
-        for s in range(64):
-            Q, i = divmod(s, 16)
-            mm2(Q, i)
-            if s > 0:
-                evac2((s - 1) // 16, (s - 1) % 16)
-            if Q < 3 and i % 4 == 1:
-                G2 = i // 4
-                unit_u(Q + 1, G2, 100)
-        evac2(3, 15)
+        for step in range(64):
+            multiply_2(step)
+            if step > 0:
+                store_2(step - 1)
+            if step < 48 and step % 4 == 1:
+                prepare_u(step // 16 + 1, (step % 16) // 4, STAGE1_BEATS)
+        store_2(63)

from contextlib import ExitStack

import concourse.mybir as mybir
from concourse.masks import make_identity

FLOPS = 2 * 2048 * 8192 * 2048 + 2 * 2048 * 2048 * 5120

F32 = mybir.dt.float32
BF16 = mybir.dt.bfloat16
U32 = mybir.dt.uint32
I32 = mybir.dt.int32
U8 = mybir.dt.uint8
FP8 = mybir.dt.float8_e4m3fn_x4
ALU = mybir.AluOpType
ACT = mybir.ActivationFunctionType

P = 128
TWO_PI = 6.283185307179586
ROPE_BASE = 10000.0

HALF_QUADS = 32
FIRST_BEAT = -2
HEAD_BEATS = 32
STAGE1_BEATS = 80
SORT_FROM = 10

KIB = 1024
X_CODES = 0
X_PLANES = X_CODES + 128 * KIB
L_CODES = X_PLANES + 8 * KIB
L_PLANES = L_CODES + 32 * KIB
W_CODES = L_PLANES + 2 * KIB
W_PLANES = W_CODES + 40 * KIB
W_RAW = W_PLANES + 5 * 512
GROUPED = W_RAW + 8 * KIB
L_BF16 = GROUPED + 12 * KIB
IDENTITY = L_BF16 + 4 * KIB
WARM = IDENTITY + 512
X_RAW = L_CODES + 8 * KIB
W_RAW_LATE = L_CODES + 24 * KIB
W_RAW_FIRST = X_CODES + 96 * KIB
GROUPED_FIRST = X_CODES + 64 * KIB
X_SORTED = X_CODES + 112 * KIB
U_RAW = 0
U_CODES_0 = 20 * KIB
COS_TABLE = 41 * KIB + 512
SIN_TABLE = COS_TABLE + 8 * KIB
ROPE_TMP = SIN_TABLE + 8 * KIB
U_CODES_1 = 64 * KIB
U_CODES_STEP = 21 * KIB + 512

ROPE, CONTENT, VALUE = (128, 64, 1024), (0, 128, 0), (192, 128, 512)


def w_unit_beat(G, g):
    quad, place = divmod(g, 4)
    first = HEAD_BEATS + 16 * (G - 1)
    if G == 0:
        return 2 * quad - 2 + place // 2
    if G == 1 and quad == 0:
        return (11, 13, 19, 21)[place]
    if G == 1:
        return first - 4 + 2 * quad + place // 2
    if quad == 0:
        return first - 15 + 2 * place
    return first - 6 + (10 * (g - 4)) // 12


def tile_multilatentattention_pa_l_kernel(tc, x, w_down, w_up, out_k, out_v):
    nc = tc.nc
    x_rows = x.flatten_outer_dims()
    k_rows = out_k.rearrange("b s h d -> (b s) (h d)")
    v_rows = out_v.rearrange("b s h d -> (b s) (h d)")

    with ExitStack() as ctx:
        sbuf_pool = ctx.enter_context(tc.tile_pool(name="sb", bufs=1))
        psum_pool = ctx.enter_context(tc.psum_pool(name="ps", bufs=1))
        ctx.enter_context(tc.manual_schedule())

        def sb(shape, dtype, offset, tag):
            return sbuf_pool.tile(shape, dtype, name=tag, tag=tag, offset=offset, align_bytes=64)

        def bank(shape, number):
            return psum_pool.tile(shape, F32, name="b%d" % number, tag="b%d" % number)

        def copy(engine, out, in_):
            if engine == "V":
                nc.vector.tensor_copy(out=out, in_=in_)
            else:
                nc.scalar.copy(out=out, in_=in_)

        count = {"grouped": 0, "l_bf16": 0, "l_quantised": 0}
        x_raw, x_sorted, x_turned, x_grouped, x_codes, x_planes = {}, {}, {}, {}, {}, {}
        w_raw, w_grouped, w_codes, w_planes = {}, {}, {}, {}
        l_sums, l_bf16, l_grouped, l_codes, l_planes = {}, {}, {}, {}, {}
        u_raw, u_codes, u_planes = {}, {}, {}
        rope, out_sums = {}, {}

        w_units_of_beat = {}
        for b in range(FIRST_BEAT, STAGE1_BEATS):
            w_units_of_beat[b] = []
        for G in range(4):
            for g in range(16):
                w_units_of_beat[w_unit_beat(G, g)].append((G, g))
        w_order = []
        for b in range(FIRST_BEAT, STAGE1_BEATS):
            w_order.extend(w_units_of_beat[b])

        def new_grouped(b):
            turn = count["grouped"]
            count["grouped"] = turn + 1
            if b < 8:
                return sb([P, 2048], BF16, GROUPED_FIRST + 4 * KIB * (turn % 8), "gra%d" % (turn % 8))
            slots = 3 if b < HEAD_BEATS else 2
            return sb([P, 2048], BF16, GROUPED + 4 * KIB * (turn % slots), "gr%d" % (turn % slots))

        def load_x(n):
            chunk, part = divmod(n, 8)
            raw = sb([P, 4, 1024], BF16, X_RAW + 8 * KIB * (n % 3), "xr%d" % (n % 3))
            rows = x_rows[512 * chunk:512 * (chunk + 1), 1024 * part:1024 * (part + 1)]
            rows = rows.rearrange("(i p) k -> p i k", p=P)
            if n == 0:
                for token_tile in range(4):
                    nc.sync.dma_start(out=raw[:, token_tile, :], in_=rows[:, token_tile, :])
            else:
                nc.sync.dma_start(out=raw[:], in_=rows)
            x_raw[n] = raw

        def sort_x(n):
            if n < 30:
                ordered = sb([P, 8, 2, P], F32, X_SORTED + 8 * KIB * (n % 2), "xq%d" % (n % 2))
            else:
                ordered = sb([P, 8, 2, P], F32, W_CODES + 8 * KIB * (n - 30), "xq%d" % (n - 28))
            words = x_raw[n][:].rearrange("p i k -> p (i k)").bitcast(F32)
            nc.vector.tensor_copy(out=ordered[:], in_=words.rearrange("p (q w u) -> p q u w", u=2, w=P))
            x_sorted[n] = ordered

        def transpose_x(n):
            for o in range(2):
                for half in range(2):
                    turned = bank([P, 2, 256], 4 + 2 * o + half)
                    for side in range(2):
                        token_tile = 2 * half + side
                        for u in range(2):
                            if n in x_sorted:
                                words = x_sorted[n][:, 2 * token_tile + o, u, :]
                            else:
                                words = x_raw[n][:, token_tile, :].bitcast(F32)[:, 256 * o + u:256 * (o + 1):2]
                            nc.tensor.transpose(turned[:, u, P * side:P * (side + 1)], words, identity[:])
                    x_turned[(n, o, half)] = turned

        def copy_x(n, o, half, engine, b):
            if (n, o) not in x_grouped:
                x_grouped[(n, o)] = new_grouped(b)
            words = x_grouped[(n, o)][:].bitcast(F32).rearrange("p (r u) -> p r u", u=2)
            copy(engine, words[:, 256 * half:256 * (half + 1), :], x_turned[(n, o, half)][:].rearrange("p u r -> p r u"))

        def quantise_x(n, o):
            chunk, part = divmod(n, 8)
            quad, later = divmod(part, 2)
            place = 2 * later + o
            if (chunk, quad) not in x_codes:
                number = 4 * chunk + quad
                x_codes[(chunk, quad)] = sb([P, 4, 512], U32, X_CODES + 8 * KIB * number, "xc%d" % number)
                x_planes[(chunk, quad)] = sb([P, 512], U8, X_PLANES + 512 * number, "xs%d" % number)
            nc.vector.quantize_mx(
                out=x_codes[(chunk, quad)][:, place, :].bitcast(FP8),
                scales=x_planes[(chunk, quad)][4 * place:P, :],
                in_=x_grouped[(n, o)][:],
            )

        def load_w(number):
            G, g = w_order[number]
            if G == 0:
                raw = sb([P, 4, 512], BF16, W_RAW_FIRST + 4 * KIB * (number % 8), "wra%d" % (number % 8))
            elif number < 20:
                raw = sb([P, 4, 512], BF16, W_RAW + 4 * KIB * (number % 2), "wr%d" % (number % 2))
            else:
                offset = (W_RAW, W_RAW + 4 * KIB, W_RAW_LATE, W_RAW_LATE + 4 * KIB)[number % 4]
                raw = sb([P, 4, 512], BF16, offset, "wr%d" % (number % 4))
            rows = w_down[512 * g:512 * (g + 1), 512 * G:512 * (G + 1)]
            nc.sync.dma_start(out=raw[:], in_=rows.rearrange("(p j) c -> p j c", j=4))
            w_raw[(G, g)] = raw

        def interleave_w(G, g, engine, b):
            grouped = new_grouped(b)
            w_grouped[(G, g)] = grouped
            copy(
                engine,
                grouped[:].rearrange("p (t m j) -> p t m j", t=4, j=4),
                w_raw[(G, g)][:].rearrange("p j (m t) -> p t m j", t=4),
            )
            number = w_order.index((G, g))
            if number < 10:
                load_w(number + 6)
            elif 14 <= number < 18:
                load_w(number + 2)
            elif 20 <= number < 60:
                load_w(number + 4)

        def quantise_w(G, g):
            quad, place = divmod(g, 4)
            if (G, quad) not in w_codes:
                slot = (4 * G + quad) % 5
                w_codes[(G, quad)] = sb([P, 4, 512], U32, W_CODES + 8 * KIB * slot, "wc%d" % slot)
                w_planes[(G, quad)] = sb([P, 512], U8, W_PLANES + 512 * slot, "ws%d" % slot)
            nc.vector.quantize_mx(
                out=w_codes[(G, quad)][:, place, :].bitcast(FP8),
                scales=w_planes[(G, quad)][4 * place:P, :],
                in_=w_grouped[(G, g)][:],
            )

        def multiply_1(G, chunk, quad, t, bank_number):
            if quad == 0:
                l_sums[(G, chunk, t)] = bank([P, 512], bank_number)
            for place in range(4):
                nc.tensor.matmul_mx(
                    out=l_sums[(G, chunk, t)][:],
                    lhsT=w_codes[(G, quad)][:, place, P * t:P * (t + 1)].bitcast(FP8),
                    lhsT_scale=w_planes[(G, quad)][4 * place:P, P * t:P * (t + 1)],
                    rhs=x_codes[(chunk, quad)][:, place, :].bitcast(FP8),
                    rhs_scale=x_planes[(chunk, quad)][4 * place:P, :],
                    start=(quad == 0 and place == 0),
                    stop=(quad == 3 and place == 3),
                )

        def round_latent(G, chunk, t, b):
            if (G, chunk) not in l_bf16:
                turn = count["l_bf16"]
                count["l_bf16"] = turn + 1
                if b < HEAD_BEATS or turn % 2 == 0:
                    l_bf16[(G, chunk)] = sb([P, 4, 512], BF16, L_BF16, "lb0")
                else:
                    l_bf16[(G, chunk)] = sb([P, 4, 512], BF16, GROUPED + 8 * KIB, "lb1")
            nc.scalar.copy(out=l_bf16[(G, chunk)][:, t, :], in_=l_sums[(G, chunk, t)][:])

        latent_waiting = []

        def interleave_latent(G, chunk, b):
            grouped = new_grouped(b)
            l_grouped[(G, chunk)] = grouped
            nc.vector.tensor_copy(
                out=grouped[:].rearrange("p (r t) -> p r t", t=4), in_=l_bf16[(G, chunk)][:].rearrange("p t r -> p r t")
            )
            latent_waiting.append((G, chunk))

        def quantise_latent():
            done = count["l_quantised"]
            if done < len(latent_waiting):
                G, chunk = latent_waiting[done]
                count["l_quantised"] = done + 1
                number = 4 * G + chunk
                l_codes[(G, chunk)] = sb([P, 512], U32, L_CODES + 2 * KIB * number, "lc%d" % number)
                if chunk not in l_planes:
                    l_planes[chunk] = sb([P, 512], U8, L_PLANES + 512 * chunk, "ls%d" % chunk)
                nc.vector.quantize_mx(
                    out=l_codes[(G, chunk)][:].bitcast(FP8), scales=l_planes[chunk][4 * G:P, :], in_=l_grouped[(G, chunk)][:]
                )

        def load_u(number):
            Q, G = divmod(number, 4)
            raw = sb([P, 4, 1280], BF16, U_RAW + 10 * KIB * (number % 2), "ur%d" % (number % 2))
            rows = w_up[512 * G:512 * (G + 1), 1280 * Q:1280 * (Q + 1)]
            nc.sync.dma_start(out=raw[:], in_=rows.rearrange("(p t) c -> p t c", t=4))
            u_raw[(Q, G)] = raw

        def interleave_u(Q, G, part, engine, b):
            feature, features = part[0], part[1]
            grouped = new_grouped(b)
            columns = u_raw[(Q, G)][:].rearrange("p t (h w) -> p h w t", h=4)[:, :, feature:feature + features, :]
            copy(engine, grouped[:, 0:16 * features].rearrange("p (h m t) -> p h m t", h=4, t=4), columns)
            return grouped

        def quantise_u(Q, G, part, grouped):
            features, column = part[1], part[2]
            if Q not in u_codes:
                offset = U_CODES_0 if Q == 0 else U_CODES_1 + U_CODES_STEP * (Q - 1)
                u_codes[Q] = sb([P, 4, 1280], U32, offset, "uc%d" % Q)
                u_planes[Q] = sb([P, 1280], U8, offset + 20 * KIB, "us%d" % Q)
            nc.vector.quantize_mx(
                out=u_codes[Q][:, G, column:column + 4 * features].bitcast(FP8),
                scales=u_planes[Q][4 * G:P, column:column + 4 * features],
                in_=grouped[:, 0:16 * features],
            )

        def prepare_u(Q, G, b):
            content = interleave_u(Q, G, CONTENT, "V", b)
            value = interleave_u(Q, G, VALUE, "S", b)
            quantise_u(Q, G, CONTENT, content)
            rotary = interleave_u(Q, G, ROPE, "V", b)
            if 4 * Q + G + 2 < 16:
                load_u(4 * Q + G + 2)
            quantise_u(Q, G, VALUE, value)
            quantise_u(Q, G, ROPE, rotary)

        def rope_constants():
            rope["chi"] = sb([P, 32], F32, IDENTITY, "chi")
            rope["cmid"] = sb([P, 32], F32, IDENTITY + 128, "cmid")
            rope["clo"] = sb([P, 32], F32, IDENTITY + 256, "clo")
            rope["posi"] = sb([P, 8], I32, IDENTITY + 384, "posi")
            rope["posf"] = sb([P, 8], F32, IDENTITY + 448, "posf")
            for frequency in range(32):
                turns = ROPE_BASE ** (-frequency / 32.0) / TWO_PI
                high = int(turns * 2.0 ** 16) / 2.0 ** 16
                middle = int((turns - high) * 2.0 ** 30) / 2.0 ** 30
                low = int((turns - high - middle) * 2.0 ** 54) / 2.0 ** 54
                column = slice(frequency, frequency + 1)
                nc.gpsimd.memset(rope["chi"][:, column], high)
                nc.gpsimd.memset(rope["cmid"][:, column], middle)
                nc.gpsimd.memset(rope["clo"][:, column], low)
            nc.gpsimd.iota(rope["posi"][:], pattern=[[P, 8]], base=0, channel_multiplier=1)

        def rope_tables():
            position = rope["posf"]
            nc.vector.tensor_copy(out=position[:], in_=rope["posi"][:])
            tmp = [sb([P, 8, 32], F32, ROPE_TMP + KIB * number, "tmp%d" % number) for number in range(5)]
            whole = sb([P, 8, 32], I32, ROPE_TMP + KIB * 5, "tmpi")
            for s in range(8):
                nc.vector.tensor_scalar_mul(out=tmp[0][:, s, :], in0=rope["chi"][:], scalar1=position[:, s:s + 1])
                nc.vector.tensor_scalar_mul(out=tmp[1][:, s, :], in0=rope["cmid"][:], scalar1=position[:, s:s + 1])
                nc.vector.tensor_scalar_mul(out=tmp[2][:, s, :], in0=rope["clo"][:], scalar1=position[:, s:s + 1])
            nc.vector.tensor_copy(out=whole[:], in_=tmp[0][:])
            nc.vector.tensor_copy(out=tmp[3][:], in_=whole[:])
            nc.vector.tensor_tensor(out=tmp[0][:], in0=tmp[0][:], in1=tmp[3][:], op=ALU.subtract)
            nc.vector.tensor_tensor(out=tmp[1][:], in0=tmp[1][:], in1=tmp[2][:], op=ALU.add)
            nc.vector.tensor_tensor(out=tmp[0][:], in0=tmp[0][:], in1=tmp[1][:], op=ALU.add)
            nc.vector.tensor_scalar_add(out=tmp[1][:], in0=tmp[0][:], scalar1=0.25)
            nc.vector.scalar_tensor_tensor(
                out=tmp[2][:], in0=tmp[0][:], scalar=0.5, in1=tmp[0][:], op0=ALU.is_gt, op1=ALU.subtract
            )
            nc.vector.scalar_tensor_tensor(
                out=tmp[3][:], in0=tmp[1][:], scalar=0.5, in1=tmp[1][:], op0=ALU.is_gt, op1=ALU.subtract
            )
            nc.scalar.activation(out=tmp[0][:], in_=tmp[2][:], func=ACT.Sin, scale=-TWO_PI)
            nc.scalar.activation(out=tmp[1][:], in_=tmp[2][:], func=ACT.Sin, scale=TWO_PI)
            nc.scalar.activation(out=tmp[4][:], in_=tmp[3][:], func=ACT.Sin, scale=-TWO_PI)
            rope["cos"] = sb([P, 8, 8, 32], F32, COS_TABLE, "cosf")
            rope["sin"] = sb([P, 8, 8, 32], F32, SIN_TABLE, "sinf")
            for head_half in range(8):
                nc.vector.tensor_copy(out=rope["cos"][:, :, head_half, :], in_=tmp[4][:])
                nc.vector.tensor_copy(out=rope["sin"][:, :, head_half, :], in_=tmp[1 - head_half % 2][:])

        def multiply_2(step):
            Q, token_tile = divmod(step, 16)
            chunk, side = divmod(token_tile, 4)
            sums = []
            for number, part in enumerate((ROPE, CONTENT, VALUE)):
                features, column = part[1], part[2]
                acc = bank([P, 4 * features], (3 * step + number + 4) % 8)
                for G in range(4):
                    nc.tensor.matmul_mx(
                        out=acc[:],
                        lhsT=l_codes[(G, chunk)][:, P * side:P * (side + 1)].bitcast(FP8),
                        lhsT_scale=l_planes[chunk][4 * G:P, P * side:P * (side + 1)],
                        rhs=u_codes[Q][:, G, column:column + 4 * features].bitcast(FP8),
                        rhs_scale=u_planes[Q][4 * G:P, column:column + 4 * features],
                        start=(G == 0),
                        stop=(G == 3),
                    )
                sums.append(acc)
            out_sums[step] = sums

        def store_2(step):
            Q, token_tile = divmod(step, 16)
            rotary, content, value = out_sums[step]
            slot = step % 4
            offset = W_CODES + 8 * KIB * (1 + slot)
            k_tile = sb([P, 4, 192], F32, offset, "ok%d" % slot)
            v_tile = sb([P, 512], F32, offset + 3 * KIB, "ov%d" % slot)
            straight = sb([P, 4, 2, 32], F32, offset + 5 * KIB, "ta%d" % slot)
            crossed = sb([P, 4, 2, 32], F32, offset + 6 * KIB, "tb%d" % slot)
            nc.scalar.copy(out=k_tile[:, :, 0:128], in_=content[:].rearrange("p (h m) -> p h m", h=4))
            nc.scalar.copy(out=v_tile[:], in_=value[:])
            u = rotary[:].rearrange("p (h e r) -> p h e r", h=4, e=2)
            cos = rope["cos"][:, token_tile % 8, :, :].rearrange("p (h e) r -> p h e r", e=2)
            sin = rope["sin"][:, token_tile % 8, :, :].rearrange("p (h e) r -> p h e r", e=2)
            nc.vector.tensor_tensor(out=straight[:], in0=u, in1=cos, op=ALU.mult)
            nc.vector.tensor_tensor(out=crossed[:, :, 0, :], in0=u[:, :, 1, :], in1=sin[:, :, 0, :], op=ALU.mult)
            nc.vector.tensor_tensor(out=crossed[:, :, 1, :], in0=u[:, :, 0, :], in1=sin[:, :, 1, :], op=ALU.mult)
            nc.vector.tensor_tensor(
                out=k_tile[:, :, 128:192],
                in0=straight[:].rearrange("p h e r -> p h (e r)"),
                in1=crossed[:].rearrange("p h e r -> p h (e r)"),
                op=ALU.add,
            )
            tokens = slice(P * token_tile, P * (token_tile + 1))
            nc.sync.dma_start(out=v_rows[tokens, 512 * Q:512 * (Q + 1)], in_=v_tile[:])
            nc.sync.dma_start(out=k_rows[tokens, 768 * Q:768 * (Q + 1)], in_=k_tile[:].rearrange("p h d -> p (h d)"))

        identity = sb([P, P], F32, IDENTITY, "ident")
        make_identity(nc, identity[:])

        load_x(0)
        load_w(0)
        load_w(1)
        load_x(1)
        load_w(2)
        load_w(3)
        load_x(2)
        load_w(4)
        load_w(5)

        warm = sb([P, 8], F32, WARM, "warm")
        nc.vector.memset(warm[:], 0.0)
        nc.scalar.copy(out=warm[:], in_=warm[:])

        for b in range(FIRST_BEAT, STAGE1_BEATS):
            head = b < HEAD_BEATS
            turning = b + 2 < HALF_QUADS
            units = w_units_of_beat[b]

            if turning:
                transpose_x(b + 2)
            if 0 <= b < HEAD_BEATS:
                G = 0
                chunk, rest = divmod(b, 8)
                quad, half = divmod(rest, 2)
                channel_tiles = (2 * half, 2 * half + 1)
                for t in channel_tiles:
                    multiply_1(G, chunk, quad, t, t)
            elif b >= HEAD_BEATS:
                G, rest = divmod(b - HEAD_BEATS, 16)
                G = G + 1
                pair, rest = divmod(rest, 8)
                quad, second = divmod(rest, 2)
                chunk = 2 * pair + second
                channel_tiles = (0, 1, 2, 3)
                for t in channel_tiles:
                    multiply_1(G, chunk, quad, t, 4 * (1 - second) + t)

            if b + 5 < HALF_QUADS:
                load_x(b + 5)
            if SORT_FROM <= b + 3 < HALF_QUADS:
                sort_x(b + 3)
            if turning:
                copy_x(b + 2, 0, 0, "V" if b < 8 else "S", b)
                copy_x(b + 2, 0, 1, "S", b)
                copy_x(b + 2, 1, 0, "S", b)
                copy_x(b + 2, 1, 1, "S", b)
                quantise_x(b + 2, 0)
            else:
                quantise_latent()

            for number, (unit_G, unit_g) in enumerate(units):
                if head:
                    engine = "S" if number == 0 else "V"
                else:
                    engine = "S" if unit_g % 2 == 0 else "V"
                interleave_w(unit_G, unit_g, engine, b)
                if number == 0:
                    quantise_latent()
                    if turning:
                        quantise_x(b + 2, 1)
                else:
                    quantise_w(units[number - 1][0], units[number - 1][1])
            if units:
                quantise_w(units[-1][0], units[-1][1])
            else:
                quantise_latent()
                if turning:
                    quantise_x(b + 2, 1)

            if b >= 0 and quad == 3:
                for t in channel_tiles:
                    round_latent(G, chunk, t, b)
                if not head:
                    interleave_latent(G, chunk, b)
            if 8 <= b <= HEAD_BEATS and b % 8 == 0:
                interleave_latent(0, b // 8 - 1, b)

            if b == 27:
                for number in range(20, 24):
                    load_w(number)
            if b == 30:
                rope_constants()
            if b == 71:
                load_u(0)
                load_u(1)
            if b == 72:
                rope_tables()
            if b in (73, 74, 76, 77):
                prepare_u(0, (73, 74, 76, 77).index(b), b)
        quantise_latent()

        for step in range(64):
            multiply_2(step)
            if step > 0:
                store_2(step - 1)
            if step < 48 and step % 4 == 1:
                prepare_u(step // 16 + 1, (step % 16) // 4, STAGE1_BEATS)
        store_2(63)
